import numpy as np
import ml_dtypes


def mxq(x, axis, fmt="e4m3"):
    dtype, down = {"e4m3": (ml_dtypes.float8_e4m3fn, 7), "e5m2": (ml_dtypes.float8_e5m2, 14)}[fmt]
    v = np.moveaxis(np.asarray(x, np.float32).astype(ml_dtypes.bfloat16).astype(np.float64), axis, -1)
    blocks = v.reshape(v.shape[:-1] + (-1, 32))
    amax = np.abs(blocks).max(-1, keepdims=True)
    byte = np.maximum(np.where(amax > 0, np.frexp(amax)[1] - 1 + 127, 0) - down, 1)
    scale = np.exp2(byte - 127.0)
    codes = (blocks / scale).astype(np.float32).astype(dtype).astype(np.float64)
    return np.moveaxis((codes * scale).reshape(v.shape), -1, axis)


WIDE = False


def mx_kscale(k):
    if not WIDE:
        return np.ones(k)
    levels = np.array([10, -10, 5, -5, 0])
    a = np.random.permutation(np.resize(levels, k // 512 * 4)).reshape(k // 512, 4)
    idx = np.arange(k)
    return np.exp2(a[idx // 512, idx % 128 // 32])


BF16 = ml_dtypes.bfloat16


def bf(x):
    return np.asarray(x, np.float32).astype(BF16)


def f64(x):
    return np.asarray(x).astype(np.float64)


E2M1 = np.array([0.0, 0.5, 1.0, 1.5, 2.0, 3.0, 4.0, 6.0, -0.0, -0.5, -1.0, -1.5, -2.0, -3.0, -4.0, -6.0])


def pack_weight(w, fmt):
    k, n = w.shape
    w = f64(bf(w)).reshape(k // 32, 32, n)
    amax = np.abs(w).max(1)
    if fmt == "e4m3":
        byte = np.frexp(amax)[1] - 1 + 127 - 7
    else:
        mant, ex = np.frexp(amax / 6.0)
        byte = np.where(mant > 0.5, ex, ex - 1) + 127
    byte = np.clip(np.where(amax > 0, byte, 1), 1, 254)
    scaled = (w * np.exp2(127.0 - byte)[:, None, :]).reshape(k, n).astype(np.float32)
    by_word = np.ascontiguousarray(scaled.reshape(k // 512, 128, 4, n).transpose(0, 1, 3, 2))
    if fmt == "e4m3":
        words = by_word.astype(ml_dtypes.float8_e4m3fn).view(np.uint8)
    else:
        c = by_word.astype(ml_dtypes.float4_e2m1fn).view(np.uint8) & 0xF
        words = c[..., 0::2] | (c[..., 1::2] << 4)
    return np.ascontiguousarray(words), np.ascontiguousarray(byte.astype(np.uint8).reshape(k // 512, 16, n))


def unpack_weight(words, scales, fmt):
    g, p, n, _ = words.shape
    if fmt == "e4m3":
        vals = np.ascontiguousarray(words).view(ml_dtypes.float8_e4m3fn).astype(np.float64)
    else:
        nib = np.empty((g, p, n, 4), np.uint8)
        nib[..., 0::2] = words & 0xF
        nib[..., 1::2] = words >> 4
        vals = E2M1[nib]
    vals = vals * np.repeat(np.exp2(scales.astype(np.float64) - 127.0), 8, axis=1)[..., None]
    return vals.transpose(0, 1, 3, 2).reshape(g * 512, n)

def pack4(w):
    words, scales = pack_weight(w, "e2m1")
    return words.reshape(words.shape[0], 128, -1), scales


def unpack4(words, scales):
    return unpack_weight(words.reshape(words.shape[0], 128, -1, 2), scales, "e2m1")


B, S, H, D = 2, 2048, 4, 128
DIM = H * D
EPS = 1e-6
QK_RMS = 0.004


def rmsnorm(x, w):
    var = np.mean(x * x, axis=-1, keepdims=True)
    return x * (1.0 / np.sqrt(var + EPS)) * w


def apply_rope(x, freqs_cis):
    x_ = x.reshape(B, H, S, D // 2, 1, 2)
    out = freqs_cis[..., 0] * x_[..., 0] + freqs_cis[..., 1] * x_[..., 1]
    return out.reshape(B, H, S, D)


def heads(t):
    return t.reshape(B, S, H, D).transpose(0, 2, 1, 3)


def setup_inputs():
    s = mx_kscale(DIM)
    col = np.repeat(np.array([QK_RMS, QK_RMS, 1.0]), DIM)
    hidden_states = bf(np.random.standard_normal((B, S, DIM)) * s)
    image_rotary_emb = bf(np.random.standard_normal((1, 1, S, D // 2, 2, 2)))
    words, scales = pack4(np.random.standard_normal((DIM, 3 * DIM)) * col / np.sqrt(DIM) / s[:, None])
    return {"hidden_states": hidden_states,
            "image_rotary_emb": image_rotary_emb,
            "w_qkv_words": words,
            "w_qkv_scales": scales,
            "b_qkv": bf(np.random.standard_normal(3 * DIM) * 0.5 * col),
            "norm_q_w": bf(1.0 + 0.1 * np.random.standard_normal(D)),
            "norm_k_w": bf(1.0 + 0.1 * np.random.standard_normal(D))}


def reference(hidden_states, image_rotary_emb, w_qkv_words, w_qkv_scales, b_qkv, norm_q_w, norm_k_w):
    xq = mxq(f64(hidden_states), 2, "e4m3")
    w = unpack4(w_qkv_words, w_qkv_scales).reshape(DIM, 3, DIM)
    b = f64(b_qkv).reshape(3, DIM)
    f = f64(image_rotary_emb)
    q = heads((xq @ w[:, 0]) + b[0])
    k = heads((xq @ w[:, 1]) + b[1])
    v = heads((xq @ w[:, 2]) + b[2])
    q = apply_rope(rmsnorm(q, f64(norm_q_w)), f)
    k = apply_rope(rmsnorm(k, f64(norm_k_w)), f)
    return q, k, v

@@ -1,0 +1,277 @@
+from contextlib import ExitStack
+
+import concourse.mybir as mybir
+from concourse.masks import make_identity
+
+F32 = mybir.dt.float32
+BF16 = mybir.dt.bfloat16
+I32 = mybir.dt.int32
+U32 = mybir.dt.uint32
+U8 = mybir.dt.uint8
+FP8X4 = mybir.dt.float8_e4m3fn_x4
+FP4X4 = mybir.dt.float4_e2m1fn_x4
+ACT = mybir.ActivationFunctionType
+ALU = mybir.AluOpType
+
+P = 128
+BATCH, SEQ, HEADS, HEAD_DIM = 2, 2048, 4, 128
+DIM = HEADS * HEAD_DIM
+EPS = 1e-6
+TILES = SEQ // P
+GROUP = 4
+TOKENS = GROUP * P
+ROUNDS = BATCH * TILES // GROUP
+UNITS = 2 * ROUNDS
+PAIRS = HEAD_DIM // 2
+
+FLOPS = 2 * BATCH * SEQ * DIM * 3 * DIM
+
+
+def tile_fluxsingleattention_pa_t_kernel(
+    tc,
+    hidden_states,
+    image_rotary_emb,
+    w_qkv_words,
+    w_qkv_scales,
+    b_qkv,
+    norm_q_w,
+    norm_k_w,
+    out_0,
+    out_1,
+    out_2,
+):
+    nc = tc.nc
+
+    x_view = hidden_states.rearrange("b (p j) k -> b p j k", j=TILES)
+    f_view = image_rotary_emb.rearrange("a c s n i e -> (a c s) (n i e)").rearrange(
+        "(p j) f -> p j f", j=TILES
+    )
+    qk_views = [o.rearrange("b h (p j) d -> b p h j d", j=TILES) for o in (out_0, out_1)]
+    v_view = out_2.rearrange("b h (p j) d -> b p h j d", j=TILES)
+
+    with ExitStack() as stack:
+        const = stack.enter_context(tc.tile_pool(name="const", bufs=1))
+        xq_pool = stack.enter_context(tc.tile_pool(name="xq", bufs=2))
+        tt_pool = stack.enter_context(tc.tile_pool(name="tt", bufs=2))
+        stat_pool = stack.enter_context(tc.tile_pool(name="stat", bufs=4))
+        rope_pool = stack.enter_context(tc.tile_pool(name="rope", bufs=3))
+        stage_pool = stack.enter_context(tc.tile_pool(name="stage", bufs=3))
+        v_pool = stack.enter_context(tc.tile_pool(name="vstage", bufs=2))
+        psum_x = stack.enter_context(tc.psum_pool(name="psum_x", bufs=1))
+        psum_mm = stack.enter_context(tc.psum_pool(name="psum_mm", bufs=2))
+        psum_t = stack.enter_context(tc.psum_pool(name="psum_t", bufs=4))
+        psum_v = stack.enter_context(tc.psum_pool(name="psum_v", bufs=1))
+        stack.enter_context(tc.manual_schedule())
+
+        w_words = const.tile([P, 2 * 3 * DIM], U8, align_bytes=64)
+        w_plane = const.tile([P, 3 * DIM], U8, align_bytes=64)
+        x_all = const.tile([P, BATCH, TILES, DIM], BF16)
+        f_sb = const.tile([P, TILES, 4 * PAIRS], BF16)
+        table = const.tile([P, TILES, 2, 2, HEAD_DIM], F32)
+        bias_rows = const.tile([P, P], BF16)
+        bias_col = const.tile([P, 2 * HEADS], F32)
+        bias_v = const.tile([P, DIM], BF16)
+        norm_q = const.tile([P, HEAD_DIM], BF16)
+        norm_k = const.tile([P, HEAD_DIM], BF16)
+        norm_w = [norm_q, norm_k]
+        ident_f32 = const.tile([P, P], F32)
+        ident_bf16 = const.tile([P, P], BF16)
+        eps = const.tile([P, 1], F32)
+        warm = const.tile([P, 1], F32)
+
+        nc.vector.memset(w_plane[:].bitcast(I32), 0)
+        nc.vector.memset(bias_rows[:], 0.0)
+        nc.vector.memset(eps[:], EPS)
+        nc.scalar.activation(out=warm[:], in_=eps[:], func=ACT.Sqrt)
+        make_identity(nc, ident_f32[:])
+        make_identity(nc, ident_bf16[:])
+
+        def load_x(rnd):
+            jg, b = divmod(rnd, BATCH)
+            tiles = slice(GROUP * jg, GROUP * (jg + 1))
+            nc.sync.dma_start(out=x_all[:, b, tiles, :], in_=x_view[b, :, tiles, :])
+
+        def load_f(jg):
+            tiles = slice(GROUP * jg, GROUP * (jg + 1))
+            nc.sync.dma_start(out=f_sb[:, tiles, :], in_=f_view[:, tiles, :])
+
+        scale_rows = w_qkv_scales.rearrange("g q n -> (g q) n")
+        for quad in range(4):
+            nc.sync.dma_start(
+                out=w_plane[32 * quad : 32 * quad + 4, :].bitcast(I32),
+                in_=scale_rows[4 * quad : 4 * quad + 4, :].bitcast(I32),
+            )
+        load_x(0)
+        nc.sync.dma_start(
+            out=w_words[:].bitcast(I32), in_=w_qkv_words.rearrange("g p n -> (g p) n").bitcast(I32)
+        )
+        nc.sync.dma_start(
+            out=bias_rows[0 : 2 * HEADS, :],
+            in_=b_qkv[0 : 2 * DIM].rearrange("(r d) -> r d", d=HEAD_DIM),
+        )
+        load_f(0)
+        nc.sync.dma_start(out=norm_q[:], in_=norm_q_w.partition_broadcast(P))
+        nc.sync.dma_start(out=norm_k[:], in_=norm_k_w.partition_broadcast(P))
+        nc.sync.dma_start(out=bias_v[:], in_=b_qkv[2 * DIM : 3 * DIM].partition_broadcast(P))
+        for rnd in range(1, ROUNDS):
+            load_x(rnd)
+            if rnd < TILES // GROUP:
+                load_f(rnd)
+
+        grouped_of = {}
+        codes_of = {}
+        t_t_of = {}
+
+        def make_table(tile, qk):
+            nc.gpsimd.tensor_tensor(
+                out=table[:, tile, qk, :, :].rearrange("p e (n i) -> p e n i", i=2),
+                in0=f_sb[:, tile, :].rearrange("p (n i e) -> p e n i", i=2, e=2),
+                in1=norm_w[qk][:]
+                .rearrange("p (n e) -> p e n", e=2)
+                .unsqueeze(3)
+                .to_broadcast([P, 2, PAIRS, 2]),
+                op=ALU.mult,
+            )
+
+        def transpose_x(rnd, half):
+            jg, b = divmod(rnd, BATCH)
+            if half == 0:
+                grouped_of[rnd] = xq_pool.tile([P, 4 * TOKENS], BF16, name="grouped", align_bytes=64)
+            xt = psum_x.tile([P, 2, 2, P], F32, tag="xt")
+            for jl in range(2):
+                words = x_all[:, b, GROUP * jg + 2 * half + jl, :].bitcast(F32)
+                for u in range(2):
+                    nc.tensor.transpose(xt[:, jl, u, :], words[:, u : DIM // 2 : 2], ident_f32[:])
+            pairs = grouped_of[rnd][:].bitcast(F32).rearrange("p (j r u) -> p j r u", j=GROUP, u=2)
+            nc.scalar.copy(
+                out=pairs[:, 2 * half : 2 * half + 2, :, :], in_=xt[:].rearrange("p j u r -> p j r u")
+            )
+
+        def quantise_x(rnd):
+            codes = xq_pool.tile([P, TOKENS], U32, name="codes", align_bytes=64)
+            x_plane = xq_pool.tile([P, TOKENS], U8, name="x_plane", align_bytes=64)
+            nc.vector.quantize_mx(
+                out=codes[:].bitcast(FP8X4), scales=x_plane[:], in_=grouped_of[rnd][:]
+            )
+            codes_of[rnd] = (codes, x_plane)
+
+        def project_head(unit, h):
+            rnd, qk = divmod(unit, 2)
+            codes, x_plane = codes_of[rnd]
+            col = (qk * HEADS + h) * HEAD_DIM
+            mm_t = psum_mm.tile([P, TOKENS], F32, name="mm_t")
+            nc.tensor.matmul_mx(
+                out=mm_t[:],
+                lhsT=w_words[:, 2 * col : 2 * (col + HEAD_DIM)].bitcast(FP4X4),
+                lhsT_scale=w_plane[:, col : col + HEAD_DIM],
+                rhs=codes[:].bitcast(FP8X4),
+                rhs_scale=x_plane[:],
+                start=True,
+                stop=True,
+            )
+            if h == 0:
+                t_t_of[unit] = tt_pool.tile([P, HEADS, TOKENS], F32, name="t_t")
+            nc.scalar.activation(
+                out=t_t_of[unit][:, h, :],
+                in_=mm_t[:],
+                func=ACT.Identity,
+                bias=bias_col[:, qk * HEADS + h : qk * HEADS + h + 1],
+                scale=1.0,
+            )
+
+        def norm_and_rope(unit, jl, stage):
+            rnd, qk = divmod(unit, 2)
+            tile = GROUP * (rnd // BATCH) + jl
+            t_bank = psum_t.tile([P, HEADS, HEAD_DIM], F32, name="t_bank")
+            for h in range(HEADS):
+                nc.tensor.transpose(
+                    t_bank[:, h, :], t_t_of[unit][:, h, P * jl : P * (jl + 1)], ident_f32[:]
+                )
+            squares = rope_pool.tile([P, HEADS, HEAD_DIM], BF16, name="squares")
+            ssq = stat_pool.tile([P, HEADS], F32, name="ssq")
+            for h in range(HEADS):
+                nc.scalar.activation(
+                    out=squares[:, h, :],
+                    in_=t_bank[:, h, :],
+                    func=ACT.Square,
+                    accum_out=ssq[:, h : h + 1],
+                )
+            rms = stat_pool.tile([P, HEADS], F32, name="rms")
+            nc.scalar.activation(
+                out=rms[:], in_=ssq[:], func=ACT.Sqrt, bias=eps[:], scale=1.0 / HEAD_DIM
+            )
+            rstd = stat_pool.tile([P, HEADS], F32, name="rstd")
+            nc.vector.reciprocal(out=rstd[:], in_=rms[:])
+            from_even = rope_pool.tile([P, HEADS, HEAD_DIM], F32, name="from_even")
+            from_odd = rope_pool.tile([P, HEADS, HEAD_DIM], F32, name="from_odd")
+            parts = [from_even, from_odd]
+            for h in range(HEADS):
+                feature_pairs = t_bank[:, h, :].rearrange("p (n e) -> p n e", e=2)
+                for e in range(2):
+                    nc.vector.scalar_tensor_tensor(
+                        out=parts[e][:, h, :].rearrange("p (n i) -> p n i", i=2),
+                        in0=feature_pairs[:, :, e : e + 1].to_broadcast([P, PAIRS, 2]),
+                        scalar=rstd[:, h : h + 1],
+                        in1=table[:, tile, qk, e, :].rearrange("p (n i) -> p n i", i=2),
+                        op0=ALU.mult,
+                        op1=ALU.mult,
+                    )
+            nc.gpsimd.tensor_tensor(
+                out=stage[:, :, jl, :], in0=from_even[:], in1=from_odd[:], op=ALU.add
+            )
+
+        def value_tile(rnd, jl, v_stage):
+            codes, x_plane = codes_of[rnd]
+            v_bank = psum_v.tile([P, DIM], F32, name="v_bank")
+            nc.tensor.matmul_mx(
+                out=v_bank[:],
+                lhsT=codes[:, P * jl : P * (jl + 1)].bitcast(FP8X4),
+                lhsT_scale=x_plane[:, P * jl : P * (jl + 1)],
+                rhs=w_words[:, 2 * 2 * DIM : 2 * 3 * DIM].bitcast(FP4X4),
+                rhs_scale=w_plane[:, 2 * DIM : 3 * DIM],
+                start=True,
+                stop=True,
+            )
+            nc.vector.tensor_tensor(
+                out=v_stage[:, :, jl, :],
+                in0=v_bank[:].rearrange("p (h d) -> p h d", h=HEADS),
+                in1=bias_v[:].rearrange("p (h d) -> p h d", h=HEADS),
+                op=ALU.add,
+            )
+
+        for qk in range(2):
+            for jl in range(GROUP):
+                make_table(jl, qk)
+        transpose_x(0, 0)
+        transpose_x(0, 1)
+        quantise_x(0)
+        bias_ps = psum_x.tile([P, P], BF16, tag="xt")
+        nc.tensor.transpose(bias_ps[:], bias_rows[:], ident_bf16[:])
+        nc.vector.tensor_copy(out=bias_col[:], in_=bias_ps[:, 0 : 2 * HEADS])
+        for h in range(HEADS):
+            project_head(0, h)
+
+        for unit in range(UNITS):
+            rnd, qk = divmod(unit, 2)
+            jg, b = divmod(rnd, BATCH)
+            tiles = slice(GROUP * jg, GROUP * (jg + 1))
+            stage = stage_pool.tile([P, HEADS, GROUP, HEAD_DIM], F32, name="stage")
+            v_stage = None
+            if qk == 1:
+                v_stage = v_pool.tile([P, HEADS, GROUP, HEAD_DIM], F32, name="v_stage")
+            for jl in range(GROUP):
+                if unit + 1 < UNITS:
+                    project_head(unit + 1, jl)
+                if qk == 1:
+                    value_tile(rnd, jl, v_stage)
+                norm_and_rope(unit, jl, stage)
+                if qk == 0 and rnd + 1 < ROUNDS:
+                    if jl < 2:
+                        transpose_x(rnd + 1, jl)
+                    if jl == 2:
+                        quantise_x(rnd + 1)
+                if b == 0 and jg + 1 < TILES // GROUP:
+                    make_table(GROUP * (jg + 1) + jl, qk)
+            nc.sync.dma_start(out=qk_views[qk][b, :, :, tiles, :], in_=stage[:])
+            if qk == 1:
+                nc.sync.dma_start(out=v_view[b, :, :, tiles, :], in_=v_stage[:])

@@ -54,14 +54,12 @@ def tile_fluxsingleattention_pa_t_kernel(
         xq_pool = stack.enter_context(tc.tile_pool(name="xq", bufs=2))
         tt_pool = stack.enter_context(tc.tile_pool(name="tt", bufs=2))
         stat_pool = stack.enter_context(tc.tile_pool(name="stat", bufs=4))
-        rope_pool = stack.enter_context(tc.tile_pool(name="rope", bufs=3))
+        rope_pool = stack.enter_context(tc.tile_pool(name="rope", bufs=4))
         stage_pool = stack.enter_context(tc.tile_pool(name="stage", bufs=3))
         v_pool = stack.enter_context(tc.tile_pool(name="vstage", bufs=2))
-        psum_x = stack.enter_context(tc.psum_pool(name="psum_x", bufs=1))
-        psum_mm = stack.enter_context(tc.psum_pool(name="psum_mm", bufs=2))
-        psum_t = stack.enter_context(tc.psum_pool(name="psum_t", bufs=4))
-        psum_v = stack.enter_context(tc.psum_pool(name="psum_v", bufs=1))
-        stack.enter_context(tc.manual_schedule())
+        psum_mm = stack.enter_context(tc.psum_pool(name="psum_mm", bufs=1))
+        psum_side = stack.enter_context(tc.psum_pool(name="psum_side", bufs=1))
+        psum_t = stack.enter_context(tc.psum_pool(name="psum_t", bufs=6))
 
         w_words = const.tile([P, 2 * 3 * DIM], U8, align_bytes=64)
         w_plane = const.tile([P, 3 * DIM], U8, align_bytes=64)
@@ -82,7 +80,7 @@ def tile_fluxsingleattention_pa_t_kernel(
         nc.vector.memset(w_plane[:].bitcast(I32), 0)
         nc.vector.memset(bias_rows[:], 0.0)
         nc.vector.memset(eps[:], EPS)
-        nc.scalar.activation(out=warm[:], in_=eps[:], func=ACT.Sqrt)
+        nc.scalar.activation(out=warm[:], in_=eps[:], func=ACT.Abs_reciprocal_sqrt)
         make_identity(nc, ident_f32[:])
         make_identity(nc, ident_bf16[:])
 
@@ -137,11 +135,14 @@ def tile_fluxsingleattention_pa_t_kernel(
             jg, b = divmod(rnd, BATCH)
             if half == 0:
                 grouped_of[rnd] = xq_pool.tile([P, 4 * TOKENS], BF16, name="grouped", align_bytes=64)
-            xt = psum_x.tile([P, 2, 2, P], F32, tag="xt")
+            xt = psum_side.tile([P, 2, 2, P], F32, tag="side")
             for jl in range(2):
                 words = x_all[:, b, GROUP * jg + 2 * half + jl, :].bitcast(F32)
                 for u in range(2):
                     nc.tensor.transpose(xt[:, jl, u, :], words[:, u : DIM // 2 : 2], ident_f32[:])
+            return xt
+
+        def regroup_x(rnd, half, xt):
             pairs = grouped_of[rnd][:].bitcast(F32).rearrange("p (j r u) -> p j r u", j=GROUP, u=2)
             nc.scalar.copy(
                 out=pairs[:, 2 * half : 2 * half + 2, :, :], in_=xt[:].rearrange("p j u r -> p j r u")
@@ -179,9 +180,7 @@ def tile_fluxsingleattention_pa_t_kernel(
                 scale=1.0,
             )
 
-        def norm_and_rope(unit, jl, stage):
-            rnd, qk = divmod(unit, 2)
-            tile = GROUP * (rnd // BATCH) + jl
+        def sum_squares(unit, jl):
             t_bank = psum_t.tile([P, HEADS, HEAD_DIM], F32, name="t_bank")
             for h in range(HEADS):
                 nc.tensor.transpose(
@@ -196,12 +195,19 @@ def tile_fluxsingleattention_pa_t_kernel(
                     func=ACT.Square,
                     accum_out=ssq[:, h : h + 1],
                 )
-            rms = stat_pool.tile([P, HEADS], F32, name="rms")
-            nc.scalar.activation(
-                out=rms[:], in_=ssq[:], func=ACT.Sqrt, bias=eps[:], scale=1.0 / HEAD_DIM
-            )
+            return t_bank, ssq
+
+        def norm_and_rope(unit, jl, t_bank, ssq, stage):
+            rnd, qk = divmod(unit, 2)
+            tile = GROUP * (rnd // BATCH) + jl
             rstd = stat_pool.tile([P, HEADS], F32, name="rstd")
-            nc.vector.reciprocal(out=rstd[:], in_=rms[:])
+            nc.scalar.activation(
+                out=rstd[:],
+                in_=ssq[:],
+                func=ACT.Abs_reciprocal_sqrt,
+                bias=eps[:],
+                scale=1.0 / HEAD_DIM,
+            )
             from_even = rope_pool.tile([P, HEADS, HEAD_DIM], F32, name="from_even")
             from_odd = rope_pool.tile([P, HEADS, HEAD_DIM], F32, name="from_odd")
             parts = [from_even, from_odd]
@@ -222,7 +228,7 @@ def tile_fluxsingleattention_pa_t_kernel(
 
         def value_tile(rnd, jl, v_stage):
             codes, x_plane = codes_of[rnd]
-            v_bank = psum_v.tile([P, DIM], F32, name="v_bank")
+            v_bank = psum_side.tile([P, DIM], F32, tag="side")
             nc.tensor.matmul_mx(
                 out=v_bank[:],
                 lhsT=codes[:, P * jl : P * (jl + 1)].bitcast(FP8X4),
@@ -242,10 +248,10 @@ def tile_fluxsingleattention_pa_t_kernel(
         for qk in range(2):
             for jl in range(GROUP):
                 make_table(jl, qk)
-        transpose_x(0, 0)
-        transpose_x(0, 1)
+        for half in range(2):
+            regroup_x(0, half, transpose_x(0, half))
         quantise_x(0)
-        bias_ps = psum_x.tile([P, P], BF16, tag="xt")
+        bias_ps = psum_side.tile([P, P], BF16, tag="side")
         nc.tensor.transpose(bias_ps[:], bias_rows[:], ident_bf16[:])
         nc.vector.tensor_copy(out=bias_col[:], in_=bias_ps[:, 0 : 2 * HEADS])
         for h in range(HEADS):
@@ -260,18 +266,21 @@ def tile_fluxsingleattention_pa_t_kernel(
             if qk == 1:
                 v_stage = v_pool.tile([P, HEADS, GROUP, HEAD_DIM], F32, name="v_stage")
             for jl in range(GROUP):
+                prepare_x = qk == 0 and rnd + 1 < ROUNDS and jl < 2
+                xt = transpose_x(rnd + 1, jl) if prepare_x else None
+                t_bank, ssq = sum_squares(unit, jl)
                 if unit + 1 < UNITS:
                     project_head(unit + 1, jl)
                 if qk == 1:
                     value_tile(rnd, jl, v_stage)
-                norm_and_rope(unit, jl, stage)
-                if qk == 0 and rnd + 1 < ROUNDS:
-                    if jl < 2:
-                        transpose_x(rnd + 1, jl)
-                    if jl == 2:
-                        quantise_x(rnd + 1)
-                if b == 0 and jg + 1 < TILES // GROUP:
-                    make_table(GROUP * (jg + 1) + jl, qk)
+                norm_and_rope(unit, jl, t_bank, ssq, stage)
+                if prepare_x:
+                    regroup_x(rnd + 1, jl, xt)
+                if qk == 0 and rnd + 1 < ROUNDS and jl == 2:
+                    quantise_x(rnd + 1)
+                step = (b * 2 + qk) * GROUP + jl
+                if jg + 1 < TILES // GROUP and step % 2 == 0:
+                    make_table(GROUP * (jg + 1) + (step // 2) % GROUP, step // (2 * GROUP))
             nc.sync.dma_start(out=qk_views[qk][b, :, :, tiles, :], in_=stage[:])
             if qk == 1:
                 nc.sync.dma_start(out=v_view[b, :, :, tiles, :], in_=v_stage[:])

@@ -161,15 +161,16 @@ def tile_fluxsingleattention_pa_t_kernel(
             codes, x_plane = codes_of[rnd]
             col = (qk * HEADS + h) * HEAD_DIM
             mm_t = psum_mm.tile([P, TOKENS], F32, name="mm_t")
-            nc.tensor.matmul_mx(
-                out=mm_t[:],
-                lhsT=w_words[:, 2 * col : 2 * (col + HEAD_DIM)].bitcast(FP4X4),
-                lhsT_scale=w_plane[:, col : col + HEAD_DIM],
-                rhs=codes[:].bitcast(FP8X4),
-                rhs_scale=x_plane[:],
-                start=True,
-                stop=True,
-            )
+            for issue in range(2):
+                nc.tensor.matmul_mx(
+                    out=mm_t[:],
+                    lhsT=w_words[:, 2 * col : 2 * (col + HEAD_DIM)].bitcast(FP4X4),
+                    lhsT_scale=w_plane[:, col : col + HEAD_DIM],
+                    rhs=codes[:].bitcast(FP8X4),
+                    rhs_scale=x_plane[:],
+                    start=True,
+                    stop=True,
+                )
             if h == 0:
                 t_t_of[unit] = tt_pool.tile([P, HEADS, TOKENS], F32, name="t_t")
             nc.scalar.activation(

@@ -161,16 +161,15 @@ def tile_fluxsingleattention_pa_t_kernel(
             codes, x_plane = codes_of[rnd]
             col = (qk * HEADS + h) * HEAD_DIM
             mm_t = psum_mm.tile([P, TOKENS], F32, name="mm_t")
-            for issue in range(2):
-                nc.tensor.matmul_mx(
-                    out=mm_t[:],
-                    lhsT=w_words[:, 2 * col : 2 * (col + HEAD_DIM)].bitcast(FP4X4),
-                    lhsT_scale=w_plane[:, col : col + HEAD_DIM],
-                    rhs=codes[:].bitcast(FP8X4),
-                    rhs_scale=x_plane[:],
-                    start=True,
-                    stop=True,
-                )
+            nc.tensor.matmul_mx(
+                out=mm_t[:],
+                lhsT=w_words[:, 2 * col : 2 * (col + HEAD_DIM)].bitcast(FP4X4),
+                lhsT_scale=w_plane[:, col : col + HEAD_DIM],
+                rhs=codes[:].bitcast(FP8X4),
+                rhs_scale=x_plane[:],
+                start=True,
+                stop=True,
+            )
             if h == 0:
                 t_t_of[unit] = tt_pool.tile([P, HEADS, TOKENS], F32, name="t_t")
             nc.scalar.activation(
@@ -223,7 +222,7 @@ def tile_fluxsingleattention_pa_t_kernel(
                         op0=ALU.mult,
                         op1=ALU.mult,
                     )
-            nc.gpsimd.tensor_tensor(
+            nc.vector.tensor_tensor(
                 out=stage[:, :, jl, :], in0=from_even[:], in1=from_odd[:], op=ALU.add
             )
 

@@ -65,14 +65,16 @@ def tile_fluxsingleattention_pa_t_kernel(
         w_plane = const.tile([P, 3 * DIM], U8, align_bytes=64)
         x_all = const.tile([P, BATCH, TILES, DIM], BF16)
         f_sb = const.tile([P, TILES, 4 * PAIRS], BF16)
-        table = const.tile([P, TILES, 2, 2, HEAD_DIM], F32)
+        table = const.tile([P, 2, TILES, 2 * HEAD_DIM], F32)
         bias_rows = const.tile([P, P], BF16)
         bias_col = const.tile([P, 2 * HEADS], F32)
         bias_v = const.tile([P, DIM], BF16)
         norm_q = const.tile([P, HEAD_DIM], BF16)
         norm_k = const.tile([P, HEAD_DIM], BF16)
         norm_w = [norm_q, norm_k]
+        norm_wide = const.tile([P, 2, 2 * HEAD_DIM], BF16)
         ident_f32 = const.tile([P, P], F32)
+        evens_first = const.tile([P, P], F32)
         ident_bf16 = const.tile([P, P], BF16)
         eps = const.tile([P, 1], F32)
         warm = const.tile([P, 1], F32)
@@ -83,6 +85,10 @@ def tile_fluxsingleattention_pa_t_kernel(
         nc.scalar.activation(out=warm[:], in_=eps[:], func=ACT.Abs_reciprocal_sqrt)
         make_identity(nc, ident_f32[:])
         make_identity(nc, ident_bf16[:])
+        nc.vector.tensor_copy(
+            out=evens_first[:].rearrange("p (e n) -> p e n", e=2),
+            in_=ident_f32[:].rearrange("p (n e) -> p e n", e=2),
+        )
 
         def load_x(rnd):
             jg, b = divmod(rnd, BATCH)
@@ -120,14 +126,15 @@ def tile_fluxsingleattention_pa_t_kernel(
         codes_of = {}
         t_t_of = {}
 
-        def make_table(tile, qk):
+        def make_tables(jg, qk):
+            tiles = slice(GROUP * jg, GROUP * (jg + 1))
             nc.gpsimd.tensor_tensor(
-                out=table[:, tile, qk, :, :].rearrange("p e (n i) -> p e n i", i=2),
-                in0=f_sb[:, tile, :].rearrange("p (n i e) -> p e n i", i=2, e=2),
-                in1=norm_w[qk][:]
-                .rearrange("p (n e) -> p e n", e=2)
-                .unsqueeze(3)
-                .to_broadcast([P, 2, PAIRS, 2]),
+                out=table[:, qk, tiles, :].rearrange("p j (e m) -> p j e m", e=2),
+                in0=f_sb[:, tiles, :].rearrange("p j (m e) -> p j e m", e=2),
+                in1=norm_wide[:, qk, :]
+                .rearrange("p (e m) -> p e m", e=2)
+                .unsqueeze(1)
+                .to_broadcast([P, GROUP, 2, HEAD_DIM]),
                 op=ALU.mult,
             )
 
@@ -184,7 +191,7 @@ def tile_fluxsingleattention_pa_t_kernel(
             t_bank = psum_t.tile([P, HEADS, HEAD_DIM], F32, name="t_bank")
             for h in range(HEADS):
                 nc.tensor.transpose(
-                    t_bank[:, h, :], t_t_of[unit][:, h, P * jl : P * (jl + 1)], ident_f32[:]
+                    t_bank[:, h, :], t_t_of[unit][:, h, P * jl : P * (jl + 1)], evens_first[:]
                 )
             squares = rope_pool.tile([P, HEADS, HEAD_DIM], BF16, name="squares")
             ssq = stat_pool.tile([P, HEADS], F32, name="ssq")
@@ -208,22 +215,21 @@ def tile_fluxsingleattention_pa_t_kernel(
                 bias=eps[:],
                 scale=1.0 / HEAD_DIM,
             )
-            from_even = rope_pool.tile([P, HEADS, HEAD_DIM], F32, name="from_even")
-            from_odd = rope_pool.tile([P, HEADS, HEAD_DIM], F32, name="from_odd")
-            parts = [from_even, from_odd]
+            products = rope_pool.tile([P, HEADS, 2, HEAD_DIM], F32, name="products")
             for h in range(HEADS):
-                feature_pairs = t_bank[:, h, :].rearrange("p (n e) -> p n e", e=2)
-                for e in range(2):
-                    nc.vector.scalar_tensor_tensor(
-                        out=parts[e][:, h, :].rearrange("p (n i) -> p n i", i=2),
-                        in0=feature_pairs[:, :, e : e + 1].to_broadcast([P, PAIRS, 2]),
-                        scalar=rstd[:, h : h + 1],
-                        in1=table[:, tile, qk, e, :].rearrange("p (n i) -> p n i", i=2),
-                        op0=ALU.mult,
-                        op1=ALU.mult,
-                    )
-            nc.vector.tensor_tensor(
-                out=stage[:, :, jl, :], in0=from_even[:], in1=from_odd[:], op=ALU.add
+                nc.vector.scalar_tensor_tensor(
+                    out=products[:, h, :, :].rearrange("p e (n i) -> p e n i", i=2),
+                    in0=t_bank[:, h, :]
+                    .rearrange("p (e n) -> p e n", e=2)
+                    .unsqueeze(3)
+                    .to_broadcast([P, 2, PAIRS, 2]),
+                    scalar=rstd[:, h : h + 1],
+                    in1=table[:, qk, tile, :].rearrange("p (e n i) -> p e n i", e=2, i=2),
+                    op0=ALU.mult,
+                    op1=ALU.mult,
+                )
+            nc.gpsimd.tensor_tensor(
+                out=stage[:, :, jl, :], in0=products[:, :, 0, :], in1=products[:, :, 1, :], op=ALU.add
             )
 
         def value_tile(rnd, jl, v_stage):
@@ -246,8 +252,14 @@ def tile_fluxsingleattention_pa_t_kernel(
             )
 
         for qk in range(2):
-            for jl in range(GROUP):
-                make_table(jl, qk)
+            nc.vector.tensor_copy(
+                out=norm_wide[:, qk, :].rearrange("p (e n i) -> p e n i", e=2, i=2),
+                in_=norm_w[qk][:]
+                .rearrange("p (n e) -> p e n", e=2)
+                .unsqueeze(3)
+                .to_broadcast([P, 2, PAIRS, 2]),
+            )
+            make_tables(0, qk)
         for half in range(2):
             regroup_x(0, half, transpose_x(0, half))
         quantise_x(0)
@@ -261,6 +273,8 @@ def tile_fluxsingleattention_pa_t_kernel(
             rnd, qk = divmod(unit, 2)
             jg, b = divmod(rnd, BATCH)
             tiles = slice(GROUP * jg, GROUP * (jg + 1))
+            if b == 0 and jg + 1 < TILES // GROUP:
+                make_tables(jg + 1, qk)
             stage = stage_pool.tile([P, HEADS, GROUP, HEAD_DIM], F32, name="stage")
             v_stage = None
             if qk == 1:
@@ -278,9 +292,6 @@ def tile_fluxsingleattention_pa_t_kernel(
                     regroup_x(rnd + 1, jl, xt)
                 if qk == 0 and rnd + 1 < ROUNDS and jl == 2:
                     quantise_x(rnd + 1)
-                step = (b * 2 + qk) * GROUP + jl
-                if jg + 1 < TILES // GROUP and step % 2 == 0:
-                    make_table(GROUP * (jg + 1) + (step // 2) % GROUP, step // (2 * GROUP))
             nc.sync.dma_start(out=qk_views[qk][b, :, :, tiles, :], in_=stage[:])
             if qk == 1:
                 nc.sync.dma_start(out=v_view[b, :, :, tiles, :], in_=v_stage[:])

@@ -228,7 +228,8 @@ def tile_fluxsingleattention_pa_t_kernel(
                     op0=ALU.mult,
                     op1=ALU.mult,
                 )
-            nc.gpsimd.tensor_tensor(
+            adder = nc.vector if jl == GROUP - 1 else nc.gpsimd
+            adder.tensor_tensor(
                 out=stage[:, :, jl, :], in0=products[:, :, 0, :], in1=products[:, :, 1, :], op=ALU.add
             )
 

@@ -23,6 +23,7 @@ TOKENS = GROUP * P
 ROUNDS = BATCH * TILES // GROUP
 UNITS = 2 * ROUNDS
 PAIRS = HEAD_DIM // 2
+ADD_TILES = 2
 
 FLOPS = 2 * BATCH * SEQ * DIM * 3 * DIM
 
@@ -55,6 +56,7 @@ def tile_fluxsingleattention_pa_t_kernel(
         tt_pool = stack.enter_context(tc.tile_pool(name="tt", bufs=2))
         stat_pool = stack.enter_context(tc.tile_pool(name="stat", bufs=4))
         rope_pool = stack.enter_context(tc.tile_pool(name="rope", bufs=4))
+        prod_pool = stack.enter_context(tc.tile_pool(name="prod", bufs=3))
         stage_pool = stack.enter_context(tc.tile_pool(name="stage", bufs=3))
         v_pool = stack.enter_context(tc.tile_pool(name="vstage", bufs=2))
         psum_mm = stack.enter_context(tc.psum_pool(name="psum_mm", bufs=1))
@@ -204,7 +206,7 @@ def tile_fluxsingleattention_pa_t_kernel(
                 )
             return t_bank, ssq
 
-        def norm_and_rope(unit, jl, t_bank, ssq, stage):
+        def norm_and_rope(unit, jl, t_bank, ssq, stage, products):
             rnd, qk = divmod(unit, 2)
             tile = GROUP * (rnd // BATCH) + jl
             rstd = stat_pool.tile([P, HEADS], F32, name="rstd")
@@ -215,10 +217,9 @@ def tile_fluxsingleattention_pa_t_kernel(
                 bias=eps[:],
                 scale=1.0 / HEAD_DIM,
             )
-            products = rope_pool.tile([P, HEADS, 2, HEAD_DIM], F32, name="products")
             for h in range(HEADS):
                 nc.vector.scalar_tensor_tensor(
-                    out=products[:, h, :, :].rearrange("p e (n i) -> p e n i", i=2),
+                    out=products[:, :, h, jl % ADD_TILES, :].rearrange("p e (n i) -> p e n i", i=2),
                     in0=t_bank[:, h, :]
                     .rearrange("p (e n) -> p e n", e=2)
                     .unsqueeze(3)
@@ -228,10 +229,13 @@ def tile_fluxsingleattention_pa_t_kernel(
                     op0=ALU.mult,
                     op1=ALU.mult,
                 )
-            adder = nc.vector if jl == GROUP - 1 else nc.gpsimd
-            adder.tensor_tensor(
-                out=stage[:, :, jl, :], in0=products[:, :, 0, :], in1=products[:, :, 1, :], op=ALU.add
-            )
+            if jl % ADD_TILES == ADD_TILES - 1:
+                nc.gpsimd.tensor_tensor(
+                    out=stage[:, :, jl + 1 - ADD_TILES : jl + 1, :],
+                    in0=products[:, 0, :, :, :],
+                    in1=products[:, 1, :, :, :],
+                    op=ALU.add,
+                )
 
         def value_tile(rnd, jl, v_stage):
             codes, x_plane = codes_of[rnd]
@@ -274,13 +278,16 @@ def tile_fluxsingleattention_pa_t_kernel(
             rnd, qk = divmod(unit, 2)
             jg, b = divmod(rnd, BATCH)
             tiles = slice(GROUP * jg, GROUP * (jg + 1))
-            if b == 0 and jg + 1 < TILES // GROUP:
-                make_tables(jg + 1, qk)
+            if qk == 0 and jg + 1 < TILES // GROUP:
+                make_tables(jg + 1, b)
             stage = stage_pool.tile([P, HEADS, GROUP, HEAD_DIM], F32, name="stage")
             v_stage = None
             if qk == 1:
                 v_stage = v_pool.tile([P, HEADS, GROUP, HEAD_DIM], F32, name="v_stage")
+            products = None
             for jl in range(GROUP):
+                if jl % ADD_TILES == 0:
+                    products = prod_pool.tile([P, 2, HEADS, ADD_TILES, HEAD_DIM], F32, name="products")
                 prepare_x = qk == 0 and rnd + 1 < ROUNDS and jl < 2
                 xt = transpose_x(rnd + 1, jl) if prepare_x else None
                 t_bank, ssq = sum_squares(unit, jl)
@@ -288,7 +295,7 @@ def tile_fluxsingleattention_pa_t_kernel(
                     project_head(unit + 1, jl)
                 if qk == 1:
                     value_tile(rnd, jl, v_stage)
-                norm_and_rope(unit, jl, t_bank, ssq, stage)
+                norm_and_rope(unit, jl, t_bank, ssq, stage, products)
                 if prepare_x:
                     regroup_x(rnd + 1, jl, xt)
                 if qk == 0 and rnd + 1 < ROUNDS and jl == 2:

@@ -59,9 +59,10 @@ def tile_fluxsingleattention_pa_t_kernel(
         prod_pool = stack.enter_context(tc.tile_pool(name="prod", bufs=3))
         stage_pool = stack.enter_context(tc.tile_pool(name="stage", bufs=3))
         v_pool = stack.enter_context(tc.tile_pool(name="vstage", bufs=2))
-        psum_mm = stack.enter_context(tc.psum_pool(name="psum_mm", bufs=1))
-        psum_side = stack.enter_context(tc.psum_pool(name="psum_side", bufs=1))
-        psum_t = stack.enter_context(tc.psum_pool(name="psum_t", bufs=6))
+        ft_pool = stack.enter_context(tc.tile_pool(name="ft", bufs=2))
+        psum_mm = stack.enter_context(tc.psum_pool(name="psum_mm", bufs=2))
+        psum_side = stack.enter_context(tc.psum_pool(name="psum_side", bufs=2))
+        psum_t = stack.enter_context(tc.psum_pool(name="psum_t", bufs=4))
 
         w_words = const.tile([P, 2 * 3 * DIM], U8, align_bytes=64)
         w_plane = const.tile([P, 3 * DIM], U8, align_bytes=64)
@@ -78,6 +79,8 @@ def tile_fluxsingleattention_pa_t_kernel(
         ident_f32 = const.tile([P, P], F32)
         evens_first = const.tile([P, P], F32)
         ident_bf16 = const.tile([P, P], BF16)
+        sorter = const.tile([P, 2, 2 * HEAD_DIM], BF16)
+        weigher = const.tile([P, 2, 2, 2 * HEAD_DIM], BF16)
         eps = const.tile([P, 1], F32)
         warm = const.tile([P, 1], F32)
 
@@ -127,6 +130,7 @@ def tile_fluxsingleattention_pa_t_kernel(
         grouped_of = {}
         codes_of = {}
         t_t_of = {}
+        f_t_of = {}
 
         def make_tables(jg, qk):
             tiles = slice(GROUP * jg, GROUP * (jg + 1))
@@ -139,6 +143,31 @@ def tile_fluxsingleattention_pa_t_kernel(
                 .to_broadcast([P, GROUP, 2, HEAD_DIM]),
                 op=ALU.mult,
             )
+
+        def transpose_f(jg):
+            ft_ps = psum_side.tile([P, 2, GROUP, P], BF16, tag="side")
+            for half in range(2):
+                for jl in range(GROUP):
+                    nc.tensor.transpose(
+                        ft_ps[:, half, jl, :],
+                        f_sb[:, GROUP * jg + jl, P * half : P * (half + 1)],
+                        ident_bf16[:],
+                    )
+            f_t = ft_pool.tile([P, 2, GROUP, P], BF16, name="f_t")
+            nc.scalar.copy(out=f_t[:], in_=ft_ps[:])
+            return f_t
+
+        def weigh_tables(jg, jl, f_t):
+            tb_ps = psum_side.tile([P, 2, 2 * HEAD_DIM], F32, tag="side")
+            for half in range(2):
+                nc.tensor.matmul(
+                    out=tb_ps[:].rearrange("p a m -> p (a m)"),
+                    lhsT=f_t[:, half, jl, :],
+                    rhs=weigher[:, half, :, :].rearrange("p a m -> p (a m)"),
+                    start=(half == 0),
+                    stop=(half == 1),
+                )
+            nc.scalar.copy(out=table[:, :, GROUP * jg + jl, :], in_=tb_ps[:])
 
         def transpose_x(rnd, half):
             jg, b = divmod(rnd, BATCH)
@@ -265,6 +294,20 @@ def tile_fluxsingleattention_pa_t_kernel(
                 .to_broadcast([P, 2, PAIRS, 2]),
             )
             make_tables(0, qk)
+        nc.gpsimd.memset(sorter[:], 0.0)
+        for half in range(2):
+            nc.gpsimd.tensor_copy(
+                out=sorter[:, half, :].rearrange("p (e n i) -> p e n i", e=2, i=2)[
+                    :, :, PAIRS // 2 * half : PAIRS // 2 * (half + 1), :
+                ],
+                in_=ident_bf16[:].rearrange("p (n i e) -> p e n i", i=2, e=2),
+            )
+            nc.gpsimd.tensor_tensor(
+                out=weigher[:, half, :, :],
+                in0=sorter[:, half, :].unsqueeze(1).to_broadcast([P, 2, 2 * HEAD_DIM]),
+                in1=norm_wide[:],
+                op=ALU.mult,
+            )
         for half in range(2):
             regroup_x(0, half, transpose_x(0, half))
         quantise_x(0)
@@ -278,8 +321,10 @@ def tile_fluxsingleattention_pa_t_kernel(
             rnd, qk = divmod(unit, 2)
             jg, b = divmod(rnd, BATCH)
             tiles = slice(GROUP * jg, GROUP * (jg + 1))
-            if qk == 0 and jg + 1 < TILES // GROUP:
-                make_tables(jg + 1, b)
+            if jg + 1 < TILES // GROUP:
+                if unit % 4 == 0:
+                    f_t_of[jg + 1] = transpose_f(jg + 1)
+                weigh_tables(jg + 1, unit % 4, f_t_of[jg + 1])
             stage = stage_pool.tile([P, HEADS, GROUP, HEAD_DIM], F32, name="stage")
             v_stage = None
             if qk == 1:

@@ -53,6 +53,7 @@ def tile_fluxsingleattention_pa_t_kernel(
     with ExitStack() as stack:
         const = stack.enter_context(tc.tile_pool(name="const", bufs=1))
         xq_pool = stack.enter_context(tc.tile_pool(name="xq", bufs=2))
+        codes_pool = stack.enter_context(tc.tile_pool(name="codes", bufs=3))
         tt_pool = stack.enter_context(tc.tile_pool(name="tt", bufs=2))
         stat_pool = stack.enter_context(tc.tile_pool(name="stat", bufs=4))
         rope_pool = stack.enter_context(tc.tile_pool(name="rope", bufs=4))
@@ -134,7 +135,7 @@ def tile_fluxsingleattention_pa_t_kernel(
 
         def make_tables(jg, qk):
             tiles = slice(GROUP * jg, GROUP * (jg + 1))
-            nc.gpsimd.tensor_tensor(
+            nc.vector.tensor_tensor(
                 out=table[:, qk, tiles, :].rearrange("p j (e m) -> p j e m", e=2),
                 in0=f_sb[:, tiles, :].rearrange("p j (m e) -> p j e m", e=2),
                 in1=norm_wide[:, qk, :]
@@ -187,8 +188,8 @@ def tile_fluxsingleattention_pa_t_kernel(
             )
 
         def quantise_x(rnd):
-            codes = xq_pool.tile([P, TOKENS], U32, name="codes", align_bytes=64)
-            x_plane = xq_pool.tile([P, TOKENS], U8, name="x_plane", align_bytes=64)
+            codes = codes_pool.tile([P, TOKENS], U32, name="codes", align_bytes=64)
+            x_plane = codes_pool.tile([P, TOKENS], U8, name="x_plane", align_bytes=64)
             nc.vector.quantize_mx(
                 out=codes[:].bitcast(FP8X4), scales=x_plane[:], in_=grouped_of[rnd][:]
             )
@@ -235,7 +236,7 @@ def tile_fluxsingleattention_pa_t_kernel(
                 )
             return t_bank, ssq
 
-        def norm_and_rope(unit, jl, t_bank, ssq, stage, products):
+        def norm_and_rope(unit, jl, t_bank, ssq, stage, products, quantise_round):
             rnd, qk = divmod(unit, 2)
             tile = GROUP * (rnd // BATCH) + jl
             rstd = stat_pool.tile([P, HEADS], F32, name="rstd")
@@ -247,6 +248,8 @@ def tile_fluxsingleattention_pa_t_kernel(
                 scale=1.0 / HEAD_DIM,
             )
             for h in range(HEADS):
+                if h == HEADS - 1 and quantise_round is not None:
+                    quantise_x(quantise_round)
                 nc.vector.scalar_tensor_tensor(
                     out=products[:, :, h, jl % ADD_TILES, :].rearrange("p e (n i) -> p e n i", i=2),
                     in0=t_bank[:, h, :]
@@ -259,7 +262,8 @@ def tile_fluxsingleattention_pa_t_kernel(
                     op1=ALU.mult,
                 )
             if jl % ADD_TILES == ADD_TILES - 1:
-                nc.gpsimd.tensor_tensor(
+                adder = nc.vector if unit == UNITS - 1 else nc.gpsimd
+                adder.tensor_tensor(
                     out=stage[:, :, jl + 1 - ADD_TILES : jl + 1, :],
                     in0=products[:, 0, :, :, :],
                     in1=products[:, 1, :, :, :],
@@ -285,6 +289,12 @@ def tile_fluxsingleattention_pa_t_kernel(
                 op=ALU.add,
             )
 
+        for half in range(2):
+            regroup_x(0, half, transpose_x(0, half))
+        quantise_x(0)
+        bias_ps = psum_side.tile([P, P], BF16, tag="side")
+        nc.tensor.transpose(bias_ps[:], bias_rows[:], ident_bf16[:])
+        nc.vector.tensor_copy(out=bias_col[:], in_=bias_ps[:, 0 : 2 * HEADS])
         for qk in range(2):
             nc.vector.tensor_copy(
                 out=norm_wide[:, qk, :].rearrange("p (e n i) -> p e n i", e=2, i=2),
@@ -293,29 +303,27 @@ def tile_fluxsingleattention_pa_t_kernel(
                 .unsqueeze(3)
                 .to_broadcast([P, 2, PAIRS, 2]),
             )
-            make_tables(0, qk)
-        nc.gpsimd.memset(sorter[:], 0.0)
+        make_tables(0, 0)
+        for h in range(HEADS):
+            project_head(0, h)
         for half in range(2):
-            nc.gpsimd.tensor_copy(
+            regroup_x(1, half, transpose_x(1, half))
+        quantise_x(1)
+        nc.vector.memset(sorter[:], 0.0)
+        for half in range(2):
+            nc.vector.tensor_copy(
                 out=sorter[:, half, :].rearrange("p (e n i) -> p e n i", e=2, i=2)[
                     :, :, PAIRS // 2 * half : PAIRS // 2 * (half + 1), :
                 ],
                 in_=ident_bf16[:].rearrange("p (n i e) -> p e n i", i=2, e=2),
             )
-            nc.gpsimd.tensor_tensor(
+            nc.vector.tensor_tensor(
                 out=weigher[:, half, :, :],
                 in0=sorter[:, half, :].unsqueeze(1).to_broadcast([P, 2, 2 * HEAD_DIM]),
                 in1=norm_wide[:],
                 op=ALU.mult,
             )
-        for half in range(2):
-            regroup_x(0, half, transpose_x(0, half))
-        quantise_x(0)
-        bias_ps = psum_side.tile([P, P], BF16, tag="side")
-        nc.tensor.transpose(bias_ps[:], bias_rows[:], ident_bf16[:])
-        nc.vector.tensor_copy(out=bias_col[:], in_=bias_ps[:, 0 : 2 * HEADS])
-        for h in range(HEADS):
-            project_head(0, h)
+        make_tables(0, 1)
 
         for unit in range(UNITS):
             rnd, qk = divmod(unit, 2)
@@ -327,24 +335,32 @@ def tile_fluxsingleattention_pa_t_kernel(
                 weigh_tables(jg + 1, unit % 4, f_t_of[jg + 1])
             stage = stage_pool.tile([P, HEADS, GROUP, HEAD_DIM], F32, name="stage")
             v_stage = None
-            if qk == 1:
+            if qk == 0:
                 v_stage = v_pool.tile([P, HEADS, GROUP, HEAD_DIM], F32, name="v_stage")
             products = None
             for jl in range(GROUP):
                 if jl % ADD_TILES == 0:
                     products = prod_pool.tile([P, 2, HEADS, ADD_TILES, HEAD_DIM], F32, name="products")
-                prepare_x = qk == 0 and rnd + 1 < ROUNDS and jl < 2
-                xt = transpose_x(rnd + 1, jl) if prepare_x else None
+                prepare_x = qk == 0 and rnd + 2 < ROUNDS and jl < 2
+                xt = transpose_x(rnd + 2, jl) if prepare_x else None
                 t_bank, ssq = sum_squares(unit, jl)
                 if unit + 1 < UNITS:
                     project_head(unit + 1, jl)
-                if qk == 1:
+                if qk == 0:
                     value_tile(rnd, jl, v_stage)
-                norm_and_rope(unit, jl, t_bank, ssq, stage, products)
+                quantise_now = qk == 0 and rnd + 2 < ROUNDS and jl == GROUP - 1
+                norm_and_rope(
+                    unit, jl, t_bank, ssq, stage, products, rnd + 2 if quantise_now else None
+                )
                 if prepare_x:
-                    regroup_x(rnd + 1, jl, xt)
-                if qk == 0 and rnd + 1 < ROUNDS and jl == 2:
-                    quantise_x(rnd + 1)
-            nc.sync.dma_start(out=qk_views[qk][b, :, :, tiles, :], in_=stage[:])
-            if qk == 1:
-                nc.sync.dma_start(out=v_view[b, :, :, tiles, :], in_=v_stage[:])
+                    regroup_x(rnd + 2, jl, xt)
+                if unit == UNITS - 1 and jl % ADD_TILES == ADD_TILES - 1:
+                    done = slice(jl + 1 - ADD_TILES, jl + 1)
+                    nc.sync.dma_start(
+                        out=qk_views[qk][b, :, :, GROUP * jg + done.start : GROUP * jg + done.stop, :],
+                        in_=stage[:, :, done, :],
+                    )
+                if qk == 0 and jl == GROUP - 1:
+                    nc.sync.dma_start(out=v_view[b, :, :, tiles, :], in_=v_stage[:])
+            if unit < UNITS - 1:
+                nc.sync.dma_start(out=qk_views[qk][b, :, :, tiles, :], in_=stage[:])

@@ -91,7 +91,7 @@ def tile_fluxsingleattention_pa_t_kernel(
         nc.scalar.activation(out=warm[:], in_=eps[:], func=ACT.Abs_reciprocal_sqrt)
         make_identity(nc, ident_f32[:])
         make_identity(nc, ident_bf16[:])
-        nc.vector.tensor_copy(
+        nc.scalar.copy(
             out=evens_first[:].rearrange("p (e n) -> p e n", e=2),
             in_=ident_f32[:].rearrange("p (n e) -> p e n", e=2),
         )
@@ -105,13 +105,16 @@ def tile_fluxsingleattention_pa_t_kernel(
             tiles = slice(GROUP * jg, GROUP * (jg + 1))
             nc.sync.dma_start(out=f_sb[:, tiles, :], in_=f_view[:, tiles, :])
 
+        nc.sync.dma_start(out=norm_q[:], in_=norm_q_w.partition_broadcast(P))
+        nc.sync.dma_start(out=norm_k[:], in_=norm_k_w.partition_broadcast(P))
+        load_f(0)
+        load_x(0)
         scale_rows = w_qkv_scales.rearrange("g q n -> (g q) n")
         for quad in range(4):
             nc.sync.dma_start(
                 out=w_plane[32 * quad : 32 * quad + 4, :].bitcast(I32),
                 in_=scale_rows[4 * quad : 4 * quad + 4, :].bitcast(I32),
             )
-        load_x(0)
         nc.sync.dma_start(
             out=w_words[:].bitcast(I32), in_=w_qkv_words.rearrange("g p n -> (g p) n").bitcast(I32)
         )
@@ -119,9 +122,6 @@ def tile_fluxsingleattention_pa_t_kernel(
             out=bias_rows[0 : 2 * HEADS, :],
             in_=b_qkv[0 : 2 * DIM].rearrange("(r d) -> r d", d=HEAD_DIM),
         )
-        load_f(0)
-        nc.sync.dma_start(out=norm_q[:], in_=norm_q_w.partition_broadcast(P))
-        nc.sync.dma_start(out=norm_k[:], in_=norm_k_w.partition_broadcast(P))
         nc.sync.dma_start(out=bias_v[:], in_=b_qkv[2 * DIM : 3 * DIM].partition_broadcast(P))
         for rnd in range(1, ROUNDS):
             load_x(rnd)
@@ -261,9 +261,8 @@ def tile_fluxsingleattention_pa_t_kernel(
                     op0=ALU.mult,
                     op1=ALU.mult,
                 )
-            if jl % ADD_TILES == ADD_TILES - 1:
-                adder = nc.vector if unit == UNITS - 1 else nc.gpsimd
-                adder.tensor_tensor(
+            if jl % ADD_TILES == ADD_TILES - 1 and (unit, jl) != (UNITS - 1, GROUP - 1):
+                nc.gpsimd.tensor_tensor(
                     out=stage[:, :, jl + 1 - ADD_TILES : jl + 1, :],
                     in0=products[:, 0, :, :, :],
                     in1=products[:, 1, :, :, :],
@@ -296,7 +295,7 @@ def tile_fluxsingleattention_pa_t_kernel(
         nc.tensor.transpose(bias_ps[:], bias_rows[:], ident_bf16[:])
         nc.vector.tensor_copy(out=bias_col[:], in_=bias_ps[:, 0 : 2 * HEADS])
         for qk in range(2):
-            nc.vector.tensor_copy(
+            nc.scalar.copy(
                 out=norm_wide[:, qk, :].rearrange("p (e n i) -> p e n i", e=2, i=2),
                 in_=norm_w[qk][:]
                 .rearrange("p (n e) -> p e n", e=2)
@@ -311,7 +310,7 @@ def tile_fluxsingleattention_pa_t_kernel(
         quantise_x(1)
         nc.vector.memset(sorter[:], 0.0)
         for half in range(2):
-            nc.vector.tensor_copy(
+            nc.scalar.copy(
                 out=sorter[:, half, :].rearrange("p (e n i) -> p e n i", e=2, i=2)[
                     :, :, PAIRS // 2 * half : PAIRS // 2 * (half + 1), :
                 ],
@@ -329,10 +328,11 @@ def tile_fluxsingleattention_pa_t_kernel(
             rnd, qk = divmod(unit, 2)
             jg, b = divmod(rnd, BATCH)
             tiles = slice(GROUP * jg, GROUP * (jg + 1))
-            if jg + 1 < TILES // GROUP:
-                if unit % 4 == 0:
-                    f_t_of[jg + 1] = transpose_f(jg + 1)
-                weigh_tables(jg + 1, unit % 4, f_t_of[jg + 1])
+            group_made, tile_made = divmod(unit + 3, 4)
+            if unit > 0 and group_made < TILES // GROUP:
+                if tile_made == 0:
+                    f_t_of[group_made] = transpose_f(group_made)
+                weigh_tables(group_made, tile_made, f_t_of[group_made])
             stage = stage_pool.tile([P, HEADS, GROUP, HEAD_DIM], F32, name="stage")
             v_stage = None
             if qk == 0:
@@ -354,12 +354,22 @@ def tile_fluxsingleattention_pa_t_kernel(
                 )
                 if prepare_x:
                     regroup_x(rnd + 2, jl, xt)
-                if unit == UNITS - 1 and jl % ADD_TILES == ADD_TILES - 1:
-                    done = slice(jl + 1 - ADD_TILES, jl + 1)
+                if unit == UNITS - 1 and jl == GROUP - ADD_TILES - 1:
                     nc.sync.dma_start(
-                        out=qk_views[qk][b, :, :, GROUP * jg + done.start : GROUP * jg + done.stop, :],
-                        in_=stage[:, :, done, :],
+                        out=qk_views[qk][b, :, :, GROUP * jg : GROUP * jg + jl + 1, :],
+                        in_=stage[:, :, 0 : jl + 1, :],
                     )
+                if unit == UNITS - 1 and jl == GROUP - 1:
+                    for done in range(GROUP - ADD_TILES, GROUP):
+                        nc.vector.tensor_tensor(
+                            out=stage[:, :, done, :],
+                            in0=products[:, 0, :, done % ADD_TILES, :],
+                            in1=products[:, 1, :, done % ADD_TILES, :],
+                            op=ALU.add,
+                        )
+                        nc.sync.dma_start(
+                            out=qk_views[qk][b, :, :, GROUP * jg + done, :], in_=stage[:, :, done, :]
+                        )
                 if qk == 0 and jl == GROUP - 1:
                     nc.sync.dma_start(out=v_view[b, :, :, tiles, :], in_=v_stage[:])
             if unit < UNITS - 1:

@@ -23,7 +23,17 @@ TOKENS = GROUP * P
 ROUNDS = BATCH * TILES // GROUP
 UNITS = 2 * ROUNDS
 PAIRS = HEAD_DIM // 2
-ADD_TILES = 2
+V_STEPS = ((0, 0), (0, 1), (0, 2), (0, 3))
+X_STEPS = ((0, 0), (0, 1))
+QUANT_STEP = (0, 3)
+POOL_CALLS = (((0, 1), (2, 3)), ((0, 1), (2, 3)))
+FIRST_POOL_CALLS = ((0, 1), (2, 3))
+LAST_POOL_CALLS = ((0, 1),)
+LAG = 1
+PROD_BUFS = 3
+STAGE_BUFS = 3
+BANKS = (2, 2, 4)
+TT_BUFS = 2
 
 FLOPS = 2 * BATCH * SEQ * DIM * 3 * DIM
 
@@ -54,16 +64,16 @@ def tile_fluxsingleattention_pa_t_kernel(
         const = stack.enter_context(tc.tile_pool(name="const", bufs=1))
         xq_pool = stack.enter_context(tc.tile_pool(name="xq", bufs=2))
         codes_pool = stack.enter_context(tc.tile_pool(name="codes", bufs=3))
-        tt_pool = stack.enter_context(tc.tile_pool(name="tt", bufs=2))
+        tt_pool = stack.enter_context(tc.tile_pool(name="tt", bufs=TT_BUFS))
         stat_pool = stack.enter_context(tc.tile_pool(name="stat", bufs=4))
         rope_pool = stack.enter_context(tc.tile_pool(name="rope", bufs=4))
-        prod_pool = stack.enter_context(tc.tile_pool(name="prod", bufs=3))
-        stage_pool = stack.enter_context(tc.tile_pool(name="stage", bufs=3))
+        prod_pool = stack.enter_context(tc.tile_pool(name="prod", bufs=PROD_BUFS))
+        stage_pool = stack.enter_context(tc.tile_pool(name="stage", bufs=STAGE_BUFS))
         v_pool = stack.enter_context(tc.tile_pool(name="vstage", bufs=2))
         ft_pool = stack.enter_context(tc.tile_pool(name="ft", bufs=2))
-        psum_mm = stack.enter_context(tc.psum_pool(name="psum_mm", bufs=2))
-        psum_side = stack.enter_context(tc.psum_pool(name="psum_side", bufs=2))
-        psum_t = stack.enter_context(tc.psum_pool(name="psum_t", bufs=4))
+        psum_mm = stack.enter_context(tc.psum_pool(name="psum_mm", bufs=BANKS[0]))
+        psum_side = stack.enter_context(tc.psum_pool(name="psum_side", bufs=BANKS[1]))
+        psum_t = stack.enter_context(tc.psum_pool(name="psum_t", bufs=BANKS[2]))
 
         w_words = const.tile([P, 2 * 3 * DIM], U8, align_bytes=64)
         w_plane = const.tile([P, 3 * DIM], U8, align_bytes=64)
@@ -73,9 +83,6 @@ def tile_fluxsingleattention_pa_t_kernel(
         bias_rows = const.tile([P, P], BF16)
         bias_col = const.tile([P, 2 * HEADS], F32)
         bias_v = const.tile([P, DIM], BF16)
-        norm_q = const.tile([P, HEAD_DIM], BF16)
-        norm_k = const.tile([P, HEAD_DIM], BF16)
-        norm_w = [norm_q, norm_k]
         norm_wide = const.tile([P, 2, 2 * HEAD_DIM], BF16)
         ident_f32 = const.tile([P, P], F32)
         evens_first = const.tile([P, P], F32)
@@ -105,10 +112,14 @@ def tile_fluxsingleattention_pa_t_kernel(
             tiles = slice(GROUP * jg, GROUP * (jg + 1))
             nc.sync.dma_start(out=f_sb[:, tiles, :], in_=f_view[:, tiles, :])
 
-        nc.sync.dma_start(out=norm_q[:], in_=norm_q_w.partition_broadcast(P))
-        nc.sync.dma_start(out=norm_k[:], in_=norm_k_w.partition_broadcast(P))
-        load_f(0)
-        load_x(0)
+        def load_x_tile(rnd, jl):
+            jg, b = divmod(rnd, BATCH)
+            nc.sync.dma_start(out=x_all[:, b, GROUP * jg + jl, :], in_=x_view[b, :, GROUP * jg + jl, :])
+
+        load_x_tile(0, 0)
+        nc.sync.dma_start(
+            out=w_words[:].bitcast(I32), in_=w_qkv_words.rearrange("g p n -> (g p) n").bitcast(I32)
+        )
         scale_rows = w_qkv_scales.rearrange("g q n -> (g q) n")
         for quad in range(4):
             nc.sync.dma_start(
@@ -116,13 +127,19 @@ def tile_fluxsingleattention_pa_t_kernel(
                 in_=scale_rows[4 * quad : 4 * quad + 4, :].bitcast(I32),
             )
         nc.sync.dma_start(
-            out=w_words[:].bitcast(I32), in_=w_qkv_words.rearrange("g p n -> (g p) n").bitcast(I32)
+            out=bias_rows[0 : 3 * HEADS, :], in_=b_qkv.rearrange("(r d) -> r d", d=HEAD_DIM)
         )
         nc.sync.dma_start(
-            out=bias_rows[0 : 2 * HEADS, :],
-            in_=b_qkv[0 : 2 * DIM].rearrange("(r d) -> r d", d=HEAD_DIM),
+            out=bias_rows[3 * HEADS : 3 * HEADS + 1, :], in_=norm_q_w.rearrange("(r d) -> r d", d=HEAD_DIM)
         )
-        nc.sync.dma_start(out=bias_v[:], in_=b_qkv[2 * DIM : 3 * DIM].partition_broadcast(P))
+        nc.sync.dma_start(
+            out=bias_rows[3 * HEADS + 1 : 3 * HEADS + 2, :],
+            in_=norm_k_w.rearrange("(r d) -> r d", d=HEAD_DIM),
+        )
+        load_x_tile(0, 1)
+        load_f(0)
+        load_x_tile(0, 2)
+        load_x_tile(0, 3)
         for rnd in range(1, ROUNDS):
             load_x(rnd)
             if rnd < TILES // GROUP:
@@ -236,7 +253,7 @@ def tile_fluxsingleattention_pa_t_kernel(
                 )
             return t_bank, ssq
 
-        def norm_and_rope(unit, jl, t_bank, ssq, stage, products, quantise_round):
+        def norm_and_rope(unit, jl, t_bank, ssq, products, slot, quantise_round):
             rnd, qk = divmod(unit, 2)
             tile = GROUP * (rnd // BATCH) + jl
             rstd = stat_pool.tile([P, HEADS], F32, name="rstd")
@@ -251,7 +268,7 @@ def tile_fluxsingleattention_pa_t_kernel(
                 if h == HEADS - 1 and quantise_round is not None:
                     quantise_x(quantise_round)
                 nc.vector.scalar_tensor_tensor(
-                    out=products[:, :, h, jl % ADD_TILES, :].rearrange("p e (n i) -> p e n i", i=2),
+                    out=products[:, :, h, slot, :].rearrange("p e (n i) -> p e n i", i=2),
                     in0=t_bank[:, h, :]
                     .rearrange("p (e n) -> p e n", e=2)
                     .unsqueeze(3)
@@ -261,13 +278,14 @@ def tile_fluxsingleattention_pa_t_kernel(
                     op0=ALU.mult,
                     op1=ALU.mult,
                 )
-            if jl % ADD_TILES == ADD_TILES - 1 and (unit, jl) != (UNITS - 1, GROUP - 1):
-                nc.gpsimd.tensor_tensor(
-                    out=stage[:, :, jl + 1 - ADD_TILES : jl + 1, :],
-                    in0=products[:, 0, :, :, :],
-                    in1=products[:, 1, :, :, :],
-                    op=ALU.add,
-                )
+
+        def add_products(engine, stage, products, first, count):
+            engine.tensor_tensor(
+                out=stage[:, :, first : first + count, :],
+                in0=products[:, 0, :, :, :],
+                in1=products[:, 1, :, :, :],
+                op=ALU.add,
+            )
 
         def value_tile(rnd, jl, v_stage):
             codes, x_plane = codes_of[rnd]
@@ -288,23 +306,94 @@ def tile_fluxsingleattention_pa_t_kernel(
                 op=ALU.add,
             )
 
-        for half in range(2):
-            regroup_x(0, half, transpose_x(0, half))
-        quantise_x(0)
-        bias_ps = psum_side.tile([P, P], BF16, tag="side")
+        def transpose_x_tile(rnd, jl):
+            jg, b = divmod(rnd, BATCH)
+            if jl == 0:
+                grouped_of[rnd] = xq_pool.tile([P, 4 * TOKENS], BF16, name="grouped", align_bytes=64)
+            xt = psum_side.tile([P, 2, P], F32, tag="side")
+            words = x_all[:, b, GROUP * jg + jl, :].bitcast(F32)
+            for u in range(2):
+                nc.tensor.transpose(xt[:, u, :], words[:, u : DIM // 2 : 2], ident_f32[:])
+            return xt
+
+        def regroup_x_tile(rnd, jl, xt):
+            pairs = grouped_of[rnd][:].bitcast(F32).rearrange("p (j r u) -> p j r u", j=GROUP, u=2)
+            nc.scalar.copy(out=pairs[:, jl, :, :], in_=xt[:].rearrange("p u r -> p r u"))
+
+        def quantise_x_tile(rnd, jl):
+            if jl == 0:
+                codes_new = codes_pool.tile([P, TOKENS], U32, name="codes", align_bytes=64)
+                plane_new = codes_pool.tile([P, TOKENS], U8, name="x_plane", align_bytes=64)
+                codes_of[rnd] = (codes_new, plane_new)
+            codes, x_plane = codes_of[rnd]
+            nc.vector.quantize_mx(
+                out=codes[:, P * jl : P * (jl + 1)].bitcast(FP8X4),
+                scales=x_plane[:, P * jl : P * (jl + 1)],
+                in_=grouped_of[rnd][:, 4 * P * jl : 4 * P * (jl + 1)],
+            )
+
+        def project_tile(unit, jl):
+            rnd, qk = divmod(unit, 2)
+            codes, x_plane = codes_of[rnd]
+            if jl == 0:
+                t_t_of[unit] = tt_pool.tile([P, HEADS, TOKENS], F32, name="t_t")
+            mm_t = psum_mm.tile([P, HEADS, P], F32, name="mm_t")
+            for h in range(HEADS):
+                col = (qk * HEADS + h) * HEAD_DIM
+                nc.tensor.matmul_mx(
+                    out=mm_t[:, h, :],
+                    lhsT=w_words[:, 2 * col : 2 * (col + HEAD_DIM)].bitcast(FP4X4),
+                    lhsT_scale=w_plane[:, col : col + HEAD_DIM],
+                    rhs=codes[:, P * jl : P * (jl + 1)].bitcast(FP8X4),
+                    rhs_scale=x_plane[:, P * jl : P * (jl + 1)],
+                    start=True,
+                    stop=True,
+                )
+            for h in range(HEADS):
+                nc.scalar.activation(
+                    out=t_t_of[unit][:, h, P * jl : P * (jl + 1)],
+                    in_=mm_t[:, h, :],
+                    func=ACT.Identity,
+                    bias=bias_col[:, qk * HEADS + h : qk * HEADS + h + 1],
+                    scale=1.0,
+                )
+
+        def spread_row(row, out):
+            nc.tensor.matmul(
+                out=out,
+                lhsT=ident_bf16[:, row : row + 1].to_broadcast([P, P]),
+                rhs=bias_rows[:],
+                start=True,
+                stop=True,
+            )
+
+        regroup_x_tile(0, 0, transpose_x_tile(0, 0))
+        quantise_x_tile(0, 0)
+        bias_ps = psum_t.tile([P, P], BF16, name="t_bank")
         nc.tensor.transpose(bias_ps[:], bias_rows[:], ident_bf16[:])
         nc.vector.tensor_copy(out=bias_col[:], in_=bias_ps[:, 0 : 2 * HEADS])
+        project_tile(0, 0)
+        norm_ps = psum_t.tile([P, 2, HEAD_DIM], F32, name="t_bank")
+        for qk in range(2):
+            spread_row(3 * HEADS + qk, norm_ps[:, qk, :])
         for qk in range(2):
             nc.scalar.copy(
                 out=norm_wide[:, qk, :].rearrange("p (e n i) -> p e n i", e=2, i=2),
-                in_=norm_w[qk][:]
+                in_=norm_ps[:, qk, :]
                 .rearrange("p (n e) -> p e n", e=2)
                 .unsqueeze(3)
                 .to_broadcast([P, 2, PAIRS, 2]),
             )
         make_tables(0, 0)
-        for h in range(HEADS):
-            project_head(0, h)
+        for jl in range(1, GROUP):
+            regroup_x_tile(0, jl, transpose_x_tile(0, jl))
+            quantise_x_tile(0, jl)
+            project_tile(0, jl)
+            if jl == 1:
+                bias_v_ps = psum_t.tile([P, HEADS, HEAD_DIM], F32, name="t_bank")
+                for h in range(HEADS):
+                    spread_row(2 * HEADS + h, bias_v_ps[:, h, :])
+                nc.scalar.copy(out=bias_v[:], in_=bias_v_ps[:].rearrange("p h d -> p (h d)"))
         for half in range(2):
             regroup_x(1, half, transpose_x(1, half))
         quantise_x(1)
@@ -324,6 +413,17 @@ def tile_fluxsingleattention_pa_t_kernel(
             )
         make_tables(0, 1)
 
+        v_stage_of = {}
+        waiting = []
+        step = 0
+
+        def flush(upto):
+            while waiting and waiting[0][0] <= upto:
+                made, stage_w, products_w, first_w, store_w = waiting.pop(0)
+                add_products(nc.vector, stage_w, products_w, first_w, 1)
+                for out_ap, in_ap in store_w:
+                    nc.sync.dma_start(out=out_ap, in_=in_ap)
+
         for unit in range(UNITS):
             rnd, qk = divmod(unit, 2)
             jg, b = divmod(rnd, BATCH)
@@ -334,43 +434,56 @@ def tile_fluxsingleattention_pa_t_kernel(
                     f_t_of[group_made] = transpose_f(group_made)
                 weigh_tables(group_made, tile_made, f_t_of[group_made])
             stage = stage_pool.tile([P, HEADS, GROUP, HEAD_DIM], F32, name="stage")
-            v_stage = None
             if qk == 0:
-                v_stage = v_pool.tile([P, HEADS, GROUP, HEAD_DIM], F32, name="v_stage")
+                v_stage_of[rnd] = v_pool.tile([P, HEADS, GROUP, HEAD_DIM], F32, name="v_stage")
+            v_stage = v_stage_of[rnd]
+            last = unit == UNITS - 1
+            calls = LAST_POOL_CALLS if last else (FIRST_POOL_CALLS if unit == 0 else POOL_CALLS[qk])
+            call_of = {}
+            for call in calls:
+                for member in call:
+                    call_of[member] = call
+            vector_tiles = [jl for jl in range(GROUP) if jl not in call_of]
             products = None
             for jl in range(GROUP):
-                if jl % ADD_TILES == 0:
-                    products = prod_pool.tile([P, 2, HEADS, ADD_TILES, HEAD_DIM], F32, name="products")
-                prepare_x = qk == 0 and rnd + 2 < ROUNDS and jl < 2
-                xt = transpose_x(rnd + 2, jl) if prepare_x else None
+                call = call_of.get(jl, (jl,))
+                if jl == call[0]:
+                    products = prod_pool.tile([P, 2, HEADS, len(call), HEAD_DIM], F32, name="products")
+                prepare_x = rnd + 2 < ROUNDS and (qk, jl) in X_STEPS
+                half = X_STEPS.index((qk, jl)) if prepare_x else None
+                xt = transpose_x(rnd + 2, half) if prepare_x else None
                 t_bank, ssq = sum_squares(unit, jl)
                 if unit + 1 < UNITS:
                     project_head(unit + 1, jl)
-                if qk == 0:
-                    value_tile(rnd, jl, v_stage)
-                quantise_now = qk == 0 and rnd + 2 < ROUNDS and jl == GROUP - 1
+                if (qk, jl) in V_STEPS:
+                    value_tile(rnd, V_STEPS.index((qk, jl)), v_stage)
+                quantise_now = rnd + 2 < ROUNDS and (qk, jl) == QUANT_STEP
                 norm_and_rope(
-                    unit, jl, t_bank, ssq, stage, products, rnd + 2 if quantise_now else None
+                    unit, jl, t_bank, ssq, products, jl - call[0], rnd + 2 if quantise_now else None
                 )
                 if prepare_x:
-                    regroup_x(rnd + 2, jl, xt)
-                if unit == UNITS - 1 and jl == GROUP - ADD_TILES - 1:
-                    nc.sync.dma_start(
-                        out=qk_views[qk][b, :, :, GROUP * jg : GROUP * jg + jl + 1, :],
-                        in_=stage[:, :, 0 : jl + 1, :],
-                    )
-                if unit == UNITS - 1 and jl == GROUP - 1:
-                    for done in range(GROUP - ADD_TILES, GROUP):
-                        nc.vector.tensor_tensor(
-                            out=stage[:, :, done, :],
-                            in0=products[:, 0, :, done % ADD_TILES, :],
-                            in1=products[:, 1, :, done % ADD_TILES, :],
-                            op=ALU.add,
-                        )
-                        nc.sync.dma_start(
-                            out=qk_views[qk][b, :, :, GROUP * jg + done, :], in_=stage[:, :, done, :]
-                        )
-                if qk == 0 and jl == GROUP - 1:
+                    regroup_x(rnd + 2, half, xt)
+                if not last:
+                    flush(step - LAG)
+                if jl in call_of:
+                    if jl == call[-1]:
+                        add_products(nc.gpsimd, stage, products, call[0], len(call))
+                        if last:
+                            nc.sync.dma_start(
+                                out=qk_views[qk][b, :, :, GROUP * jg + call[0] : GROUP * jg + jl + 1, :],
+                                in_=stage[:, :, call[0] : jl + 1, :],
+                            )
+                else:
+                    store = []
+                    if last:
+                        store = [(qk_views[qk][b, :, :, GROUP * jg + jl, :], stage[:, :, jl, :])]
+                    elif jl == vector_tiles[-1] and jl + LAG >= GROUP:
+                        store = [(qk_views[qk][b, :, :, tiles, :], stage[:])]
+                    waiting.append((step, stage, products, jl, store))
+                if (qk, jl) == V_STEPS[-1]:
                     nc.sync.dma_start(out=v_view[b, :, :, tiles, :], in_=v_stage[:])
-            if unit < UNITS - 1:
+                step += 1
+            if last:
+                flush(step)
+            elif not (vector_tiles and vector_tiles[-1] + LAG >= GROUP):
                 nc.sync.dma_start(out=qk_views[qk][b, :, :, tiles, :], in_=stage[:])

@@ -30,6 +30,9 @@ POOL_CALLS = (((0, 1), (2, 3)), ((0, 1), (2, 3)))
 FIRST_POOL_CALLS = ((0, 1), (2, 3))
 LAST_POOL_CALLS = ((0, 1),)
 LAG = 1
+REDUCE_ADD = True
+X_EARLY = True
+X_VECTOR_FROM = 3
 PROD_BUFS = 3
 STAGE_BUFS = 3
 BANKS = (2, 2, 4)
@@ -200,9 +203,14 @@ def tile_fluxsingleattention_pa_t_kernel(
 
         def regroup_x(rnd, half, xt):
             pairs = grouped_of[rnd][:].bitcast(F32).rearrange("p (j r u) -> p j r u", j=GROUP, u=2)
-            nc.scalar.copy(
-                out=pairs[:, 2 * half : 2 * half + 2, :, :], in_=xt[:].rearrange("p j u r -> p j r u")
-            )
+            if rnd >= X_VECTOR_FROM:
+                nc.vector.tensor_copy(
+                    out=pairs[:, 2 * half : 2 * half + 2, :, :], in_=xt[:].rearrange("p j u r -> p j r u")
+                )
+            else:
+                nc.scalar.copy(
+                    out=pairs[:, 2 * half : 2 * half + 2, :, :], in_=xt[:].rearrange("p j u r -> p j r u")
+                )
 
         def quantise_x(rnd):
             codes = codes_pool.tile([P, TOKENS], U32, name="codes", align_bytes=64)
@@ -413,14 +421,30 @@ def tile_fluxsingleattention_pa_t_kernel(
             )
         make_tables(0, 1)
 
+        x_steps = {(0, 0): (2, 0), (0, 1): (2, 1)}
+        for x_rnd in range(3, ROUNDS):
+            x_unit = 2 * (x_rnd - 3) + 1 if X_EARLY else 2 * (x_rnd - 2)
+            x_steps[(x_unit, 0)] = (x_rnd, 0)
+            x_steps[(x_unit, 1)] = (x_rnd, 1)
         v_stage_of = {}
         waiting = []
         step = 0
 
+        def store_w_is_last(store_w):
+            return len(store_w) == 1 and store_w[0][1].shape[2] == HEAD_DIM and len(store_w[0][1].shape) == 3
+
         def flush(upto):
             while waiting and waiting[0][0] <= upto:
                 made, stage_w, products_w, first_w, store_w = waiting.pop(0)
-                add_products(nc.vector, stage_w, products_w, first_w, 1)
+                if REDUCE_ADD and not store_w_is_last(store_w):
+                    nc.vector.tensor_reduce(
+                        out=stage_w[:, :, first_w, :],
+                        in_=products_w[:, :, :, 0, :].rearrange("p e h d -> p h d e"),
+                        axis=mybir.AxisListType.X,
+                        op=ALU.add,
+                    )
+                else:
+                    add_products(nc.vector, stage_w, products_w, first_w, 1)
                 for out_ap, in_ap in store_w:
                     nc.sync.dma_start(out=out_ap, in_=in_ap)
 
@@ -449,9 +473,9 @@ def tile_fluxsingleattention_pa_t_kernel(
                 call = call_of.get(jl, (jl,))
                 if jl == call[0]:
                     products = prod_pool.tile([P, 2, HEADS, len(call), HEAD_DIM], F32, name="products")
-                prepare_x = rnd + 2 < ROUNDS and (qk, jl) in X_STEPS
-                half = X_STEPS.index((qk, jl)) if prepare_x else None
-                xt = transpose_x(rnd + 2, half) if prepare_x else None
+                prepare_x = (unit, jl) in x_steps
+                x_round, half = x_steps.get((unit, jl), (None, None))
+                xt = transpose_x(x_round, half) if prepare_x else None
                 t_bank, ssq = sum_squares(unit, jl)
                 if unit + 1 < UNITS:
                     project_head(unit + 1, jl)
@@ -462,7 +486,7 @@ def tile_fluxsingleattention_pa_t_kernel(
                     unit, jl, t_bank, ssq, products, jl - call[0], rnd + 2 if quantise_now else None
                 )
                 if prepare_x:
-                    regroup_x(rnd + 2, half, xt)
+                    regroup_x(x_round, half, xt)
                 if not last:
                     flush(step - LAG)
                 if jl in call_of:

@@ -26,8 +26,8 @@ PAIRS = HEAD_DIM // 2
 V_STEPS = ((0, 0), (0, 1), (0, 2), (0, 3))
 X_STEPS = ((0, 0), (0, 1))
 QUANT_STEP = (0, 3)
-POOL_CALLS = (((0, 1), (2, 3)), ((0, 1), (2, 3)))
-FIRST_POOL_CALLS = ((0, 1), (2, 3))
+POOL_CALLS = (((0,), (1,), (2, 3)), ((0, 1), (2, 3)))
+FIRST_POOL_CALLS = ((0,), (1,), (2, 3))
 LAST_POOL_CALLS = ((0, 1),)
 LAG = 1
 REDUCE_ADD = True

@@ -33,7 +33,7 @@ LAG = 1
 REDUCE_ADD = True
 X_EARLY = True
 X_VECTOR_FROM = 3
-PROD_BUFS = 3
+PROD_BUFS = 5
 STAGE_BUFS = 3
 BANKS = (2, 2, 4)
 TT_BUFS = 2

from contextlib import ExitStack

import concourse.mybir as mybir
from concourse.masks import make_identity

F32 = mybir.dt.float32
BF16 = mybir.dt.bfloat16
I32 = mybir.dt.int32
U32 = mybir.dt.uint32
U8 = mybir.dt.uint8
FP8X4 = mybir.dt.float8_e4m3fn_x4
FP4X4 = mybir.dt.float4_e2m1fn_x4
ACT = mybir.ActivationFunctionType
ALU = mybir.AluOpType

P = 128
BATCH, SEQ, HEADS, HEAD_DIM = 2, 2048, 4, 128
DIM = HEADS * HEAD_DIM
EPS = 1e-6
TILES = SEQ // P
GROUP = 4
TOKENS = GROUP * P
ROUNDS = BATCH * TILES // GROUP
UNITS = 2 * ROUNDS
PAIRS = HEAD_DIM // 2
V_STEPS = ((0, 0), (0, 1), (0, 2), (0, 3))
X_STEPS = ((0, 0), (0, 1))
QUANT_STEP = (0, 3)
POOL_CALLS = (((0,), (1,), (2, 3)), ((0, 1), (2, 3)))
FIRST_POOL_CALLS = ((0,), (1,), (2, 3))
LAST_POOL_CALLS = ((0, 1),)
LAG = 1
REDUCE_ADD = True
X_EARLY = True
X_VECTOR_FROM = 3
PROD_BUFS = 5
STAGE_BUFS = 3
BANKS = (2, 2, 4)
TT_BUFS = 2

FLOPS = 2 * BATCH * SEQ * DIM * 3 * DIM


def tile_fluxsingleattention_pa_t_kernel(
    tc,
    hidden_states,
    image_rotary_emb,
    w_qkv_words,
    w_qkv_scales,
    b_qkv,
    norm_q_w,
    norm_k_w,
    out_0,
    out_1,
    out_2,
):
    nc = tc.nc

    x_view = hidden_states.rearrange("b (p j) k -> b p j k", j=TILES)
    f_view = image_rotary_emb.rearrange("a c s n i e -> (a c s) (n i e)").rearrange(
        "(p j) f -> p j f", j=TILES
    )
    qk_views = [o.rearrange("b h (p j) d -> b p h j d", j=TILES) for o in (out_0, out_1)]
    v_view = out_2.rearrange("b h (p j) d -> b p h j d", j=TILES)

    with ExitStack() as stack:
        const = stack.enter_context(tc.tile_pool(name="const", bufs=1))
        xq_pool = stack.enter_context(tc.tile_pool(name="xq", bufs=2))
        codes_pool = stack.enter_context(tc.tile_pool(name="codes", bufs=3))
        tt_pool = stack.enter_context(tc.tile_pool(name="tt", bufs=TT_BUFS))
        stat_pool = stack.enter_context(tc.tile_pool(name="stat", bufs=4))
        rope_pool = stack.enter_context(tc.tile_pool(name="rope", bufs=4))
        prod_pool = stack.enter_context(tc.tile_pool(name="prod", bufs=PROD_BUFS))
        stage_pool = stack.enter_context(tc.tile_pool(name="stage", bufs=STAGE_BUFS))
        v_pool = stack.enter_context(tc.tile_pool(name="vstage", bufs=2))
        ft_pool = stack.enter_context(tc.tile_pool(name="ft", bufs=2))
        psum_mm = stack.enter_context(tc.psum_pool(name="psum_mm", bufs=BANKS[0]))
        psum_side = stack.enter_context(tc.psum_pool(name="psum_side", bufs=BANKS[1]))
        psum_t = stack.enter_context(tc.psum_pool(name="psum_t", bufs=BANKS[2]))

        w_words = const.tile([P, 2 * 3 * DIM], U8, align_bytes=64)
        w_plane = const.tile([P, 3 * DIM], U8, align_bytes=64)
        x_all = const.tile([P, BATCH, TILES, DIM], BF16)
        f_sb = const.tile([P, TILES, 4 * PAIRS], BF16)
        table = const.tile([P, 2, TILES, 2 * HEAD_DIM], F32)
        bias_rows = const.tile([P, P], BF16)
        bias_col = const.tile([P, 2 * HEADS], F32)
        bias_v = const.tile([P, DIM], BF16)
        norm_wide = const.tile([P, 2, 2 * HEAD_DIM], BF16)
        ident_f32 = const.tile([P, P], F32)
        evens_first = const.tile([P, P], F32)
        ident_bf16 = const.tile([P, P], BF16)
        sorter = const.tile([P, 2, 2 * HEAD_DIM], BF16)
        weigher = const.tile([P, 2, 2, 2 * HEAD_DIM], BF16)
        eps = const.tile([P, 1], F32)
        warm = const.tile([P, 1], F32)

        nc.vector.memset(w_plane[:].bitcast(I32), 0)
        nc.vector.memset(bias_rows[:], 0.0)
        nc.vector.memset(eps[:], EPS)
        nc.scalar.activation(out=warm[:], in_=eps[:], func=ACT.Abs_reciprocal_sqrt)
        make_identity(nc, ident_f32[:])
        make_identity(nc, ident_bf16[:])
        nc.scalar.copy(
            out=evens_first[:].rearrange("p (e n) -> p e n", e=2),
            in_=ident_f32[:].rearrange("p (n e) -> p e n", e=2),
        )

        def load_x(rnd):
            jg, b = divmod(rnd, BATCH)
            tiles = slice(GROUP * jg, GROUP * (jg + 1))
            nc.sync.dma_start(out=x_all[:, b, tiles, :], in_=x_view[b, :, tiles, :])

        def load_f(jg):
            tiles = slice(GROUP * jg, GROUP * (jg + 1))
            nc.sync.dma_start(out=f_sb[:, tiles, :], in_=f_view[:, tiles, :])

        def load_x_tile(rnd, jl):
            jg, b = divmod(rnd, BATCH)
            nc.sync.dma_start(out=x_all[:, b, GROUP * jg + jl, :], in_=x_view[b, :, GROUP * jg + jl, :])

        load_x_tile(0, 0)
        nc.sync.dma_start(
            out=w_words[:].bitcast(I32), in_=w_qkv_words.rearrange("g p n -> (g p) n").bitcast(I32)
        )
        scale_rows = w_qkv_scales.rearrange("g q n -> (g q) n")
        for quad in range(4):
            nc.sync.dma_start(
                out=w_plane[32 * quad : 32 * quad + 4, :].bitcast(I32),
                in_=scale_rows[4 * quad : 4 * quad + 4, :].bitcast(I32),
            )
        nc.sync.dma_start(
            out=bias_rows[0 : 3 * HEADS, :], in_=b_qkv.rearrange("(r d) -> r d", d=HEAD_DIM)
        )
        nc.sync.dma_start(
            out=bias_rows[3 * HEADS : 3 * HEADS + 1, :], in_=norm_q_w.rearrange("(r d) -> r d", d=HEAD_DIM)
        )
        nc.sync.dma_start(
            out=bias_rows[3 * HEADS + 1 : 3 * HEADS + 2, :],
            in_=norm_k_w.rearrange("(r d) -> r d", d=HEAD_DIM),
        )
        load_x_tile(0, 1)
        load_f(0)
        load_x_tile(0, 2)
        load_x_tile(0, 3)
        for rnd in range(1, ROUNDS):
            load_x(rnd)
            if rnd < TILES // GROUP:
                load_f(rnd)

        grouped_of = {}
        codes_of = {}
        t_t_of = {}
        f_t_of = {}

        def make_tables(jg, qk):
            tiles = slice(GROUP * jg, GROUP * (jg + 1))
            nc.vector.tensor_tensor(
                out=table[:, qk, tiles, :].rearrange("p j (e m) -> p j e m", e=2),
                in0=f_sb[:, tiles, :].rearrange("p j (m e) -> p j e m", e=2),
                in1=norm_wide[:, qk, :]
                .rearrange("p (e m) -> p e m", e=2)
                .unsqueeze(1)
                .to_broadcast([P, GROUP, 2, HEAD_DIM]),
                op=ALU.mult,
            )

        def transpose_f(jg):
            ft_ps = psum_side.tile([P, 2, GROUP, P], BF16, tag="side")
            for half in range(2):
                for jl in range(GROUP):
                    nc.tensor.transpose(
                        ft_ps[:, half, jl, :],
                        f_sb[:, GROUP * jg + jl, P * half : P * (half + 1)],
                        ident_bf16[:],
                    )
            f_t = ft_pool.tile([P, 2, GROUP, P], BF16, name="f_t")
            nc.scalar.copy(out=f_t[:], in_=ft_ps[:])
            return f_t

        def weigh_tables(jg, jl, f_t):
            tb_ps = psum_side.tile([P, 2, 2 * HEAD_DIM], F32, tag="side")
            for half in range(2):
                nc.tensor.matmul(
                    out=tb_ps[:].rearrange("p a m -> p (a m)"),
                    lhsT=f_t[:, half, jl, :],
                    rhs=weigher[:, half, :, :].rearrange("p a m -> p (a m)"),
                    start=(half == 0),
                    stop=(half == 1),
                )
            nc.scalar.copy(out=table[:, :, GROUP * jg + jl, :], in_=tb_ps[:])

        def transpose_x(rnd, half):
            jg, b = divmod(rnd, BATCH)
            if half == 0:
                grouped_of[rnd] = xq_pool.tile([P, 4 * TOKENS], BF16, name="grouped", align_bytes=64)
            xt = psum_side.tile([P, 2, 2, P], F32, tag="side")
            for jl in range(2):
                words = x_all[:, b, GROUP * jg + 2 * half + jl, :].bitcast(F32)
                for u in range(2):
                    nc.tensor.transpose(xt[:, jl, u, :], words[:, u : DIM // 2 : 2], ident_f32[:])
            return xt

        def regroup_x(rnd, half, xt):
            pairs = grouped_of[rnd][:].bitcast(F32).rearrange("p (j r u) -> p j r u", j=GROUP, u=2)
            if rnd >= X_VECTOR_FROM:
                nc.vector.tensor_copy(
                    out=pairs[:, 2 * half : 2 * half + 2, :, :], in_=xt[:].rearrange("p j u r -> p j r u")
                )
            else:
                nc.scalar.copy(
                    out=pairs[:, 2 * half : 2 * half + 2, :, :], in_=xt[:].rearrange("p j u r -> p j r u")
                )

        def quantise_x(rnd):
            codes = codes_pool.tile([P, TOKENS], U32, name="codes", align_bytes=64)
            x_plane = codes_pool.tile([P, TOKENS], U8, name="x_plane", align_bytes=64)
            nc.vector.quantize_mx(
                out=codes[:].bitcast(FP8X4), scales=x_plane[:], in_=grouped_of[rnd][:]
            )
            codes_of[rnd] = (codes, x_plane)

        def project_head(unit, h):
            rnd, qk = divmod(unit, 2)
            codes, x_plane = codes_of[rnd]
            col = (qk * HEADS + h) * HEAD_DIM
            mm_t = psum_mm.tile([P, TOKENS], F32, name="mm_t")
            nc.tensor.matmul_mx(
                out=mm_t[:],
                lhsT=w_words[:, 2 * col : 2 * (col + HEAD_DIM)].bitcast(FP4X4),
                lhsT_scale=w_plane[:, col : col + HEAD_DIM],
                rhs=codes[:].bitcast(FP8X4),
                rhs_scale=x_plane[:],
                start=True,
                stop=True,
            )
            if h == 0:
                t_t_of[unit] = tt_pool.tile([P, HEADS, TOKENS], F32, name="t_t")
            nc.scalar.activation(
                out=t_t_of[unit][:, h, :],
                in_=mm_t[:],
                func=ACT.Identity,
                bias=bias_col[:, qk * HEADS + h : qk * HEADS + h + 1],
                scale=1.0,
            )

        def sum_squares(unit, jl):
            t_bank = psum_t.tile([P, HEADS, HEAD_DIM], F32, name="t_bank")
            for h in range(HEADS):
                nc.tensor.transpose(
                    t_bank[:, h, :], t_t_of[unit][:, h, P * jl : P * (jl + 1)], evens_first[:]
                )
            squares = rope_pool.tile([P, HEADS, HEAD_DIM], BF16, name="squares")
            ssq = stat_pool.tile([P, HEADS], F32, name="ssq")
            for h in range(HEADS):
                nc.scalar.activation(
                    out=squares[:, h, :],
                    in_=t_bank[:, h, :],
                    func=ACT.Square,
                    accum_out=ssq[:, h : h + 1],
                )
            return t_bank, ssq

        def norm_and_rope(unit, jl, t_bank, ssq, products, slot, quantise_round):
            rnd, qk = divmod(unit, 2)
            tile = GROUP * (rnd // BATCH) + jl
            rstd = stat_pool.tile([P, HEADS], F32, name="rstd")
            nc.scalar.activation(
                out=rstd[:],
                in_=ssq[:],
                func=ACT.Abs_reciprocal_sqrt,
                bias=eps[:],
                scale=1.0 / HEAD_DIM,
            )
            for h in range(HEADS):
                if h == HEADS - 1 and quantise_round is not None:
                    quantise_x(quantise_round)
                nc.vector.scalar_tensor_tensor(
                    out=products[:, :, h, slot, :].rearrange("p e (n i) -> p e n i", i=2),
                    in0=t_bank[:, h, :]
                    .rearrange("p (e n) -> p e n", e=2)
                    .unsqueeze(3)
                    .to_broadcast([P, 2, PAIRS, 2]),
                    scalar=rstd[:, h : h + 1],
                    in1=table[:, qk, tile, :].rearrange("p (e n i) -> p e n i", e=2, i=2),
                    op0=ALU.mult,
                    op1=ALU.mult,
                )

        def add_products(engine, stage, products, first, count):
            engine.tensor_tensor(
                out=stage[:, :, first : first + count, :],
                in0=products[:, 0, :, :, :],
                in1=products[:, 1, :, :, :],
                op=ALU.add,
            )

        def value_tile(rnd, jl, v_stage):
            codes, x_plane = codes_of[rnd]
            v_bank = psum_side.tile([P, DIM], F32, tag="side")
            nc.tensor.matmul_mx(
                out=v_bank[:],
                lhsT=codes[:, P * jl : P * (jl + 1)].bitcast(FP8X4),
                lhsT_scale=x_plane[:, P * jl : P * (jl + 1)],
                rhs=w_words[:, 2 * 2 * DIM : 2 * 3 * DIM].bitcast(FP4X4),
                rhs_scale=w_plane[:, 2 * DIM : 3 * DIM],
                start=True,
                stop=True,
            )
            nc.vector.tensor_tensor(
                out=v_stage[:, :, jl, :],
                in0=v_bank[:].rearrange("p (h d) -> p h d", h=HEADS),
                in1=bias_v[:].rearrange("p (h d) -> p h d", h=HEADS),
                op=ALU.add,
            )

        def transpose_x_tile(rnd, jl):
            jg, b = divmod(rnd, BATCH)
            if jl == 0:
                grouped_of[rnd] = xq_pool.tile([P, 4 * TOKENS], BF16, name="grouped", align_bytes=64)
            xt = psum_side.tile([P, 2, P], F32, tag="side")
            words = x_all[:, b, GROUP * jg + jl, :].bitcast(F32)
            for u in range(2):
                nc.tensor.transpose(xt[:, u, :], words[:, u : DIM // 2 : 2], ident_f32[:])
            return xt

        def regroup_x_tile(rnd, jl, xt):
            pairs = grouped_of[rnd][:].bitcast(F32).rearrange("p (j r u) -> p j r u", j=GROUP, u=2)
            nc.scalar.copy(out=pairs[:, jl, :, :], in_=xt[:].rearrange("p u r -> p r u"))

        def quantise_x_tile(rnd, jl):
            if jl == 0:
                codes_new = codes_pool.tile([P, TOKENS], U32, name="codes", align_bytes=64)
                plane_new = codes_pool.tile([P, TOKENS], U8, name="x_plane", align_bytes=64)
                codes_of[rnd] = (codes_new, plane_new)
            codes, x_plane = codes_of[rnd]
            nc.vector.quantize_mx(
                out=codes[:, P * jl : P * (jl + 1)].bitcast(FP8X4),
                scales=x_plane[:, P * jl : P * (jl + 1)],
                in_=grouped_of[rnd][:, 4 * P * jl : 4 * P * (jl + 1)],
            )

        def project_tile(unit, jl):
            rnd, qk = divmod(unit, 2)
            codes, x_plane = codes_of[rnd]
            if jl == 0:
                t_t_of[unit] = tt_pool.tile([P, HEADS, TOKENS], F32, name="t_t")
            mm_t = psum_mm.tile([P, HEADS, P], F32, name="mm_t")
            for h in range(HEADS):
                col = (qk * HEADS + h) * HEAD_DIM
                nc.tensor.matmul_mx(
                    out=mm_t[:, h, :],
                    lhsT=w_words[:, 2 * col : 2 * (col + HEAD_DIM)].bitcast(FP4X4),
                    lhsT_scale=w_plane[:, col : col + HEAD_DIM],
                    rhs=codes[:, P * jl : P * (jl + 1)].bitcast(FP8X4),
                    rhs_scale=x_plane[:, P * jl : P * (jl + 1)],
                    start=True,
                    stop=True,
                )
            for h in range(HEADS):
                nc.scalar.activation(
                    out=t_t_of[unit][:, h, P * jl : P * (jl + 1)],
                    in_=mm_t[:, h, :],
                    func=ACT.Identity,
                    bias=bias_col[:, qk * HEADS + h : qk * HEADS + h + 1],
                    scale=1.0,
                )

        def spread_row(row, out):
            nc.tensor.matmul(
                out=out,
                lhsT=ident_bf16[:, row : row + 1].to_broadcast([P, P]),
                rhs=bias_rows[:],
                start=True,
                stop=True,
            )

        regroup_x_tile(0, 0, transpose_x_tile(0, 0))
        quantise_x_tile(0, 0)
        bias_ps = psum_t.tile([P, P], BF16, name="t_bank")
        nc.tensor.transpose(bias_ps[:], bias_rows[:], ident_bf16[:])
        nc.vector.tensor_copy(out=bias_col[:], in_=bias_ps[:, 0 : 2 * HEADS])
        project_tile(0, 0)
        norm_ps = psum_t.tile([P, 2, HEAD_DIM], F32, name="t_bank")
        for qk in range(2):
            spread_row(3 * HEADS + qk, norm_ps[:, qk, :])
        for qk in range(2):
            nc.scalar.copy(
                out=norm_wide[:, qk, :].rearrange("p (e n i) -> p e n i", e=2, i=2),
                in_=norm_ps[:, qk, :]
                .rearrange("p (n e) -> p e n", e=2)
                .unsqueeze(3)
                .to_broadcast([P, 2, PAIRS, 2]),
            )
        make_tables(0, 0)
        for jl in range(1, GROUP):
            regroup_x_tile(0, jl, transpose_x_tile(0, jl))
            quantise_x_tile(0, jl)
            project_tile(0, jl)
            if jl == 1:
                bias_v_ps = psum_t.tile([P, HEADS, HEAD_DIM], F32, name="t_bank")
                for h in range(HEADS):
                    spread_row(2 * HEADS + h, bias_v_ps[:, h, :])
                nc.scalar.copy(out=bias_v[:], in_=bias_v_ps[:].rearrange("p h d -> p (h d)"))
        for half in range(2):
            regroup_x(1, half, transpose_x(1, half))
        quantise_x(1)
        nc.vector.memset(sorter[:], 0.0)
        for half in range(2):
            nc.scalar.copy(
                out=sorter[:, half, :].rearrange("p (e n i) -> p e n i", e=2, i=2)[
                    :, :, PAIRS // 2 * half : PAIRS // 2 * (half + 1), :
                ],
                in_=ident_bf16[:].rearrange("p (n i e) -> p e n i", i=2, e=2),
            )
            nc.vector.tensor_tensor(
                out=weigher[:, half, :, :],
                in0=sorter[:, half, :].unsqueeze(1).to_broadcast([P, 2, 2 * HEAD_DIM]),
                in1=norm_wide[:],
                op=ALU.mult,
            )
        make_tables(0, 1)

        x_steps = {(0, 0): (2, 0), (0, 1): (2, 1)}
        for x_rnd in range(3, ROUNDS):
            x_unit = 2 * (x_rnd - 3) + 1 if X_EARLY else 2 * (x_rnd - 2)
            x_steps[(x_unit, 0)] = (x_rnd, 0)
            x_steps[(x_unit, 1)] = (x_rnd, 1)
        v_stage_of = {}
        waiting = []
        step = 0

        def store_w_is_last(store_w):
            return len(store_w) == 1 and store_w[0][1].shape[2] == HEAD_DIM and len(store_w[0][1].shape) == 3

        def flush(upto):
            while waiting and waiting[0][0] <= upto:
                made, stage_w, products_w, first_w, store_w = waiting.pop(0)
                if REDUCE_ADD and not store_w_is_last(store_w):
                    nc.vector.tensor_reduce(
                        out=stage_w[:, :, first_w, :],
                        in_=products_w[:, :, :, 0, :].rearrange("p e h d -> p h d e"),
                        axis=mybir.AxisListType.X,
                        op=ALU.add,
                    )
                else:
                    add_products(nc.vector, stage_w, products_w, first_w, 1)
                for out_ap, in_ap in store_w:
                    nc.sync.dma_start(out=out_ap, in_=in_ap)

        for unit in range(UNITS):
            rnd, qk = divmod(unit, 2)
            jg, b = divmod(rnd, BATCH)
            tiles = slice(GROUP * jg, GROUP * (jg + 1))
            group_made, tile_made = divmod(unit + 3, 4)
            if unit > 0 and group_made < TILES // GROUP:
                if tile_made == 0:
                    f_t_of[group_made] = transpose_f(group_made)
                weigh_tables(group_made, tile_made, f_t_of[group_made])
            stage = stage_pool.tile([P, HEADS, GROUP, HEAD_DIM], F32, name="stage")
            if qk == 0:
                v_stage_of[rnd] = v_pool.tile([P, HEADS, GROUP, HEAD_DIM], F32, name="v_stage")
            v_stage = v_stage_of[rnd]
            last = unit == UNITS - 1
            calls = LAST_POOL_CALLS if last else (FIRST_POOL_CALLS if unit == 0 else POOL_CALLS[qk])
            call_of = {}
            for call in calls:
                for member in call:
                    call_of[member] = call
            vector_tiles = [jl for jl in range(GROUP) if jl not in call_of]
            products = None
            for jl in range(GROUP):
                call = call_of.get(jl, (jl,))
                if jl == call[0]:
                    products = prod_pool.tile([P, 2, HEADS, len(call), HEAD_DIM], F32, name="products")
                prepare_x = (unit, jl) in x_steps
                x_round, half = x_steps.get((unit, jl), (None, None))
                xt = transpose_x(x_round, half) if prepare_x else None
                t_bank, ssq = sum_squares(unit, jl)
                if unit + 1 < UNITS:
                    project_head(unit + 1, jl)
                if (qk, jl) in V_STEPS:
                    value_tile(rnd, V_STEPS.index((qk, jl)), v_stage)
                quantise_now = rnd + 2 < ROUNDS and (qk, jl) == QUANT_STEP
                norm_and_rope(
                    unit, jl, t_bank, ssq, products, jl - call[0], rnd + 2 if quantise_now else None
                )
                if prepare_x:
                    regroup_x(x_round, half, xt)
                if not last:
                    flush(step - LAG)
                if jl in call_of:
                    if jl == call[-1]:
                        add_products(nc.gpsimd, stage, products, call[0], len(call))
                        if last:
                            nc.sync.dma_start(
                                out=qk_views[qk][b, :, :, GROUP * jg + call[0] : GROUP * jg + jl + 1, :],
                                in_=stage[:, :, call[0] : jl + 1, :],
                            )
                else:
                    store = []
                    if last:
                        store = [(qk_views[qk][b, :, :, GROUP * jg + jl, :], stage[:, :, jl, :])]
                    elif jl == vector_tiles[-1] and jl + LAG >= GROUP:
                        store = [(qk_views[qk][b, :, :, tiles, :], stage[:])]
                    waiting.append((step, stage, products, jl, store))
                if (qk, jl) == V_STEPS[-1]:
                    nc.sync.dma_start(out=v_view[b, :, :, tiles, :], in_=v_stage[:])
                step += 1
            if last:
                flush(step)
            elif not (vector_tiles and vector_tiles[-1] + LAG >= GROUP):
                nc.sync.dma_start(out=qk_views[qk][b, :, :, tiles, :], in_=stage[:])
